import numpy as np
import ml_dtypes


def mxq(x, axis, fmt="e4m3"):
    dtype, down = {"e4m3": (ml_dtypes.float8_e4m3fn, 7), "e5m2": (ml_dtypes.float8_e5m2, 14)}[fmt]
    v = np.moveaxis(np.asarray(x, np.float32).astype(ml_dtypes.bfloat16).astype(np.float64), axis, -1)
    blocks = v.reshape(v.shape[:-1] + (-1, 32))
    amax = np.abs(blocks).max(-1, keepdims=True)
    byte = np.maximum(np.where(amax > 0, np.frexp(amax)[1] - 1 + 127, 0) - down, 1)
    scale = np.exp2(byte - 127.0)
    codes = (blocks / scale).astype(np.float32).astype(dtype).astype(np.float64)
    return np.moveaxis((codes * scale).reshape(v.shape), -1, axis)


WIDE = False


def mx_kscale(k):
    if not WIDE:
        return np.ones(k)
    levels = np.array([10, -10, 5, -5, 0])
    a = np.random.permutation(np.resize(levels, k // 512 * 4)).reshape(k // 512, 4)
    idx = np.arange(k)
    return np.exp2(a[idx // 512, idx % 128 // 32])


BF16 = ml_dtypes.bfloat16


def bf(x):
    return np.asarray(x, np.float32).astype(BF16)


def f64(x):
    return np.asarray(x).astype(np.float64)


E2M1 = np.array([0.0, 0.5, 1.0, 1.5, 2.0, 3.0, 4.0, 6.0, -0.0, -0.5, -1.0, -1.5, -2.0, -3.0, -4.0, -6.0])


def pack_weight(w, fmt):
    k, n = w.shape
    w = f64(bf(w)).reshape(k // 32, 32, n)
    amax = np.abs(w).max(1)
    if fmt == "e4m3":
        byte = np.frexp(amax)[1] - 1 + 127 - 7
    else:
        mant, ex = np.frexp(amax / 6.0)
        byte = np.where(mant > 0.5, ex, ex - 1) + 127
    byte = np.clip(np.where(amax > 0, byte, 1), 1, 254)
    scaled = (w * np.exp2(127.0 - byte)[:, None, :]).reshape(k, n).astype(np.float32)
    by_word = np.ascontiguousarray(scaled.reshape(k // 512, 128, 4, n).transpose(0, 1, 3, 2))
    if fmt == "e4m3":
        words = by_word.astype(ml_dtypes.float8_e4m3fn).view(np.uint8)
    else:
        c = by_word.astype(ml_dtypes.float4_e2m1fn).view(np.uint8) & 0xF
        words = c[..., 0::2] | (c[..., 1::2] << 4)
    return np.ascontiguousarray(words), np.ascontiguousarray(byte.astype(np.uint8).reshape(k // 512, 16, n))


def unpack_weight(words, scales, fmt):
    g, p, n, _ = words.shape
    if fmt == "e4m3":
        vals = np.ascontiguousarray(words).view(ml_dtypes.float8_e4m3fn).astype(np.float64)
    else:
        nib = np.empty((g, p, n, 4), np.uint8)
        nib[..., 0::2] = words & 0xF
        nib[..., 1::2] = words >> 4
        vals = E2M1[nib]
    vals = vals * np.repeat(np.exp2(scales.astype(np.float64) - 127.0), 8, axis=1)[..., None]
    return vals.transpose(0, 1, 3, 2).reshape(g * 512, n)


B, D_IN, D_H = 512, 1024, 1024
FMT = "e4m3"


def setup_inputs():
    s, t = mx_kscale(D_IN), mx_kscale(D_H)
    inp = {"x": bf(np.random.standard_normal((B, D_IN)) * s),
           "h_prev": bf(np.random.standard_normal((B, D_H)) * t),
           "c_prev": bf(np.random.standard_normal((B, D_H))),
           "n_prev": bf(np.random.uniform(size=(B, D_H)))}
    for g in ("i", "f", "z"):
        words, scales = pack_weight(np.random.standard_normal((D_IN, D_H)) * 0.5 / np.sqrt(D_IN) / s[:, None], FMT)
        inp["W_" + g + "_words"] = words
        inp["W_" + g + "_scales"] = scales
        inp["b_" + g] = bf(np.random.standard_normal(D_H) * 0.3)
        words, scales = pack_weight(np.random.standard_normal((D_H, D_H)) * 0.5 / np.sqrt(D_H) / t[:, None], FMT)
        inp["U_" + g + "_words"] = words
        inp["U_" + g + "_scales"] = scales
    return inp


def reference(x, h_prev, c_prev, n_prev, W_i_words, W_i_scales, b_i, U_i_words, U_i_scales, W_f_words, W_f_scales, b_f, U_f_words, U_f_scales, W_z_words, W_z_scales, b_z, U_z_words, U_z_scales):
    xq = mxq(f64(x), 1, "e4m3")
    hq = mxq(f64(h_prev), 1, "e4m3")
    i = np.exp((xq @ unpack_weight(W_i_words, W_i_scales, FMT)) + f64(b_i) + (hq @ unpack_weight(U_i_words, U_i_scales, FMT)))
    f = np.exp((xq @ unpack_weight(W_f_words, W_f_scales, FMT)) + f64(b_f) + (hq @ unpack_weight(U_f_words, U_f_scales, FMT)))
    z = np.tanh((xq @ unpack_weight(W_z_words, W_z_scales, FMT)) + f64(b_z) + (hq @ unpack_weight(U_z_words, U_z_scales, FMT)))
    c = f * f64(c_prev) + i * z
    n = f * f64(n_prev) + i
    return (c, n)

@@ -1,0 +1,178 @@
+from contextlib import ExitStack
+
+from concourse import mybir
+from concourse.masks import make_identity
+
+F32 = mybir.dt.float32
+BF16 = mybir.dt.bfloat16
+I32 = mybir.dt.int32
+U32 = mybir.dt.uint32
+U8 = mybir.dt.uint8
+FP8X4 = mybir.dt.float8_e4m3fn_x4
+ADD = mybir.AluOpType.add
+MULT = mybir.AluOpType.mult
+EXP = mybir.ActivationFunctionType.Exp
+TANH = mybir.ActivationFunctionType.Tanh
+
+P = 128
+BATCH = 512
+D_IN = 1024
+D_H = 1024
+K_PASS = 512
+HALVES = D_IN // K_PASS
+PASSES = 2 * HALVES
+B_TILES = BATCH // P
+N_CHUNK = 512
+N_CHUNKS = D_H // N_CHUNK
+GATES = ("f", "i", "z")
+
+FLOPS = 2 * BATCH * (2 * D_IN) * (3 * D_H)
+
+
+def tile_slstmcell_pa_kernel(
+    tc,
+    x, h_prev, c_prev, n_prev,
+    W_i_words, W_i_scales, b_i, U_i_words, U_i_scales,
+    W_f_words, W_f_scales, b_f, U_f_words, U_f_scales,
+    W_z_words, W_z_scales, b_z, U_z_words, U_z_scales,
+    out_0, out_1,
+):
+    nc = tc.nc
+    words_of = {"i": (W_i_words, U_i_words), "f": (W_f_words, U_f_words), "z": (W_z_words, U_z_words)}
+    scales_of = {"i": (W_i_scales, U_i_scales), "f": (W_f_scales, U_f_scales), "z": (W_z_scales, U_z_scales)}
+    bias_of = {"i": b_i, "f": b_f, "z": b_z}
+
+    with ExitStack() as stack:
+        keep = stack.enter_context(tc.tile_pool(name="keep", bufs=1))
+        stage = stack.enter_context(tc.tile_pool(name="stage", bufs=4))
+        work = stack.enter_context(tc.tile_pool(name="work", bufs=4))
+        state = stack.enter_context(tc.tile_pool(name="state", bufs=2 * B_TILES))
+        psum = stack.enter_context(tc.psum_pool(name="psum", bufs=1))
+
+        ident = keep.tile([P, P], F32, name="ident")
+        raw = [keep.tile([P, 2, D_IN], BF16, name="raw%d" % bt) for bt in range(B_TILES)]
+        act_codes = keep.tile([P, B_TILES, PASSES * P], U32, name="act_codes", align_bytes=64)
+        act_scales = keep.tile([P, B_TILES, PASSES * P], U8, name="act_scales", align_bytes=64)
+        w_codes = {}
+        for gate in GATES:
+            for nch in range(N_CHUNKS):
+                w_codes[gate, nch] = keep.tile(
+                    [P, PASSES, N_CHUNK], U32, name="w_%s%d" % (gate, nch), align_bytes=64
+                )
+        w_planes = {g: keep.tile([P, D_H], U8, name="planes_%s" % g, align_bytes=64) for g in GATES}
+        bias = {g: keep.tile([P, D_H], BF16, name="bias_%s" % g) for g in GATES}
+        prev = [keep.tile([P, B_TILES, 2, N_CHUNK], BF16, name="prev%d" % nch) for nch in range(N_CHUNKS)]
+
+        for gate in GATES:
+            nc.vector.memset(w_planes[gate][:].bitcast(I32), 0)
+        make_identity(nc, ident[:])
+        for gate in GATES:
+            nc.scalar.dma_start(out=bias[gate][:], in_=bias_of[gate].partition_broadcast(P))
+
+        def load_planes(gate):
+            for s in range(2):
+                for quad in range(4):
+                    first = 32 * quad + 4 * HALVES * s
+                    nc.sync.dma_start(
+                        out=w_planes[gate][first : first + 4 * HALVES, :].bitcast(I32),
+                        in_=scales_of[gate][s][:, 4 * quad : 4 * quad + 4, :].bitcast(I32),
+                    )
+
+        def load_words(gate, nch):
+            for s in range(2):
+                by_partition = words_of[gate][s].rearrange("g p n t -> p g (n t)")
+                nc.sync.dma_start(
+                    out=w_codes[gate, nch][:, HALVES * s : HALVES * (s + 1), :].bitcast(I32),
+                    in_=by_partition[:, :, 4 * N_CHUNK * nch : 4 * N_CHUNK * (nch + 1)].bitcast(I32),
+                )
+
+        def load_prev(nch):
+            cols = slice(N_CHUNK * nch, N_CHUNK * (nch + 1))
+            for row, source in enumerate((c_prev, n_prev)):
+                nc.sync.dma_start(
+                    out=prev[nch][:, :, row, :],
+                    in_=source.rearrange("(bt p) n -> p bt n", p=P)[:, :, cols],
+                )
+
+        for bt in range(B_TILES):
+            for s, source in enumerate((x, h_prev)):
+                nc.sync.dma_start(out=raw[bt][:, s, :], in_=source[P * bt : P * (bt + 1), :])
+        load_planes("f")
+        load_words("f", 0)
+        load_prev(0)
+        load_planes("i")
+        load_words("i", 0)
+        load_planes("z")
+        load_words("z", 0)
+        load_words("f", 1)
+        load_prev(1)
+        load_words("i", 1)
+        load_words("z", 1)
+
+        for bt in range(B_TILES):
+            for s in range(2):
+                pairs = raw[bt][:, s, :].bitcast(F32)
+                turned = psum.tile([P, HALVES * 2, P], F32, name="turned", tag="turned", bufs=2)
+                for g in range(HALVES):
+                    for u in range(2):
+                        nc.tensor.transpose(
+                            turned[:, 2 * g + u, :],
+                            pairs[:, 256 * g + u : 256 * (g + 1) : 2],
+                            ident[:],
+                        )
+                grouped = stage.tile([P, HALVES, P, 4], BF16, name="grouped", align_bytes=64)
+                nc.scalar.copy(
+                    out=grouped[:].bitcast(F32),
+                    in_=turned[:].rearrange("p (g u) b -> p g b u", u=2),
+                )
+                cols = slice(HALVES * P * s, HALVES * P * (s + 1))
+                nc.vector.quantize_mx(
+                    out=act_codes[:, bt, cols].bitcast(FP8X4),
+                    scales=act_scales[:, bt, cols],
+                    in_=grouped[:].rearrange("p g b t -> p (g b t)"),
+                )
+
+        for nch in range(N_CHUNKS):
+            cols = slice(N_CHUNK * nch, N_CHUNK * (nch + 1))
+            carried = [None] * B_TILES
+            added = [None] * B_TILES
+            for gate in GATES:
+                for bt in range(B_TILES):
+                    acc = psum.tile([P, N_CHUNK], F32, name="acc", tag="acc", bufs=6)
+                    for c in range(PASSES):
+                        nc.tensor.matmul_mx(
+                            out=acc[:],
+                            lhsT=act_codes[:, bt, P * c : P * (c + 1)].bitcast(FP8X4),
+                            lhsT_scale=act_scales[:, bt, P * c : P * (c + 1)],
+                            rhs=w_codes[gate, nch][:, c, :].bitcast(FP8X4),
+                            rhs_scale=w_planes[gate][4 * c : P, cols],
+                            start=(c == 0),
+                            stop=(c == PASSES - 1),
+                        )
+                    pre = work.tile([P, N_CHUNK], F32, name="pre")
+                    nc.vector.tensor_tensor(out=pre[:], in0=acc[:], in1=bias[gate][:, cols], op=ADD)
+                    if gate == "f":
+                        forget = work.tile([P, N_CHUNK], F32, name="forget")
+                        nc.scalar.activation(out=forget[:], in_=pre[:], func=EXP)
+                        carried[bt] = state.tile([P, 2, N_CHUNK], F32, name="carried")
+                        nc.vector.tensor_tensor(
+                            out=carried[bt][:],
+                            in0=forget[:].unsqueeze(1).to_broadcast([P, 2, N_CHUNK]),
+                            in1=prev[nch][:, bt, :, :],
+                            op=MULT,
+                        )
+                    elif gate == "i":
+                        added[bt] = state.tile([P, 2, N_CHUNK], F32, name="added")
+                        nc.scalar.activation(out=added[bt][:, 1, :], in_=pre[:], func=EXP)
+                    else:
+                        cell_in = work.tile([P, N_CHUNK], F32, name="cell_in")
+                        nc.scalar.activation(out=cell_in[:], in_=pre[:], func=TANH)
+                        nc.vector.tensor_tensor(
+                            out=added[bt][:, 0, :], in0=added[bt][:, 1, :], in1=cell_in[:], op=MULT
+                        )
+                        nc.vector.tensor_tensor(
+                            out=carried[bt][:], in0=carried[bt][:], in1=added[bt][:], op=ADD
+                        )
+                        rows = slice(P * bt, P * (bt + 1))
+                        nc.sync.dma_start(out=out_0[rows, cols], in_=carried[bt][:, 0, :])
+                        nc.sync.dma_start(out=out_1[rows, cols], in_=carried[bt][:, 1, :])

@@ -24,7 +24,7 @@ PASSES = 2 * HALVES
 B_TILES = BATCH // P
 N_CHUNK = 512
 N_CHUNKS = D_H // N_CHUNK
-GATES = ("f", "i", "z")
+GATES = ("i", "z", "f")
 
 FLOPS = 2 * BATCH * (2 * D_IN) * (3 * D_H)
 
@@ -50,6 +50,9 @@ def tile_slstmcell_pa_kernel(
         psum = stack.enter_context(tc.psum_pool(name="psum", bufs=1))
 
         ident = keep.tile([P, P], F32, name="ident")
+        ident_bf = keep.tile([P, P], BF16, name="ident_bf")
+        ones = keep.tile([P, P], BF16, name="ones")
+        bias_rows = keep.tile([P, len(GATES), D_H], BF16, name="bias_rows")
         raw = [keep.tile([P, 2, D_IN], BF16, name="raw%d" % bt) for bt in range(B_TILES)]
         act_codes = keep.tile([P, B_TILES, PASSES * P], U32, name="act_codes", align_bytes=64)
         act_scales = keep.tile([P, B_TILES, PASSES * P], U8, name="act_scales", align_bytes=64)
@@ -66,8 +69,13 @@ def tile_slstmcell_pa_kernel(
         for gate in GATES:
             nc.vector.memset(w_planes[gate][:].bitcast(I32), 0)
         make_identity(nc, ident[:])
-        for gate in GATES:
-            nc.scalar.dma_start(out=bias[gate][:], in_=bias_of[gate].partition_broadcast(P))
+        make_identity(nc, ident_bf[:])
+        nc.vector.memset(ones[:], 1.0)
+        nc.vector.memset(bias_rows[:].rearrange("p g n -> p (g n)").bitcast(I32), 0)
+        for gi, gate in enumerate(GATES):
+            nc.scalar.dma_start(
+                out=bias_rows[0:1, gi, :], in_=bias_of[gate].rearrange("(o n) -> o n", o=1)
+            )
 
         def load_planes(gate):
             for s in range(2):
@@ -97,22 +105,18 @@ def tile_slstmcell_pa_kernel(
         for bt in range(B_TILES):
             for s, source in enumerate((x, h_prev)):
                 nc.sync.dma_start(out=raw[bt][:, s, :], in_=source[P * bt : P * (bt + 1), :])
-        load_planes("f")
-        load_words("f", 0)
+        for gate in GATES:
+            load_planes(gate)
+            load_words(gate, 0)
         load_prev(0)
-        load_planes("i")
-        load_words("i", 0)
-        load_planes("z")
-        load_words("z", 0)
-        load_words("f", 1)
+        for gate in GATES:
+            load_words(gate, 1)
         load_prev(1)
-        load_words("i", 1)
-        load_words("z", 1)
 
         for bt in range(B_TILES):
             for s in range(2):
                 pairs = raw[bt][:, s, :].bitcast(F32)
-                turned = psum.tile([P, HALVES * 2, P], F32, name="turned", tag="turned", bufs=2)
+                turned = psum.tile([P, HALVES * 2, P], F32, name="turned", tag="aux", bufs=4)
                 for g in range(HALVES):
                     for u in range(2):
                         nc.tensor.transpose(
@@ -132,13 +136,21 @@ def tile_slstmcell_pa_kernel(
                     in_=grouped[:].rearrange("p g b t -> p (g b t)"),
                 )
 
+        for gi, gate in enumerate(GATES):
+            for nch in range(N_CHUNKS):
+                cols = slice(N_CHUNK * nch, N_CHUNK * (nch + 1))
+                spread = psum.tile([P, N_CHUNK], F32, name="spread", tag="aux", bufs=4)
+                nc.tensor.matmul(out=spread[:], lhsT=ones[:], rhs=bias_rows[:, gi, cols], start=True, stop=True)
+                nc.vector.tensor_copy(out=bias[gate][:, cols], in_=spread[:])
+
         for nch in range(N_CHUNKS):
             cols = slice(N_CHUNK * nch, N_CHUNK * (nch + 1))
-            carried = [None] * B_TILES
-            added = [None] * B_TILES
+            in_gate = [None] * B_TILES
+            fresh = [None] * B_TILES
             for gate in GATES:
                 for bt in range(B_TILES):
-                    acc = psum.tile([P, N_CHUNK], F32, name="acc", tag="acc", bufs=6)
+                    rows = slice(P * bt, P * (bt + 1))
+                    acc = psum.tile([P, N_CHUNK], F32, name="acc", tag="acc", bufs=4)
                     for c in range(PASSES):
                         nc.tensor.matmul_mx(
                             out=acc[:],
@@ -151,28 +163,25 @@ def tile_slstmcell_pa_kernel(
                         )
                     pre = work.tile([P, N_CHUNK], F32, name="pre")
                     nc.vector.tensor_tensor(out=pre[:], in0=acc[:], in1=bias[gate][:, cols], op=ADD)
-                    if gate == "f":
+                    if gate == "i":
+                        in_gate[bt] = state.tile([P, N_CHUNK], F32, name="in_gate")
+                        nc.scalar.activation(out=in_gate[bt][:], in_=pre[:], func=EXP)
+                    elif gate == "z":
+                        fresh[bt] = state.tile([P, N_CHUNK], F32, name="fresh")
+                        nc.scalar.activation(out=fresh[bt][:], in_=pre[:], func=TANH)
+                        nc.gpsimd.tensor_tensor(out=fresh[bt][:], in0=fresh[bt][:], in1=in_gate[bt][:], op=MULT)
+                    else:
                         forget = work.tile([P, N_CHUNK], F32, name="forget")
                         nc.scalar.activation(out=forget[:], in_=pre[:], func=EXP)
-                        carried[bt] = state.tile([P, 2, N_CHUNK], F32, name="carried")
-                        nc.vector.tensor_tensor(
-                            out=carried[bt][:],
-                            in0=forget[:].unsqueeze(1).to_broadcast([P, 2, N_CHUNK]),
-                            in1=prev[nch][:, bt, :, :],
-                            op=MULT,
-                        )
-                    elif gate == "i":
-                        added[bt] = state.tile([P, 2, N_CHUNK], F32, name="added")
-                        nc.scalar.activation(out=added[bt][:, 1, :], in_=pre[:], func=EXP)
-                    else:
-                        cell_in = work.tile([P, N_CHUNK], F32, name="cell_in")
-                        nc.scalar.activation(out=cell_in[:], in_=pre[:], func=TANH)
-                        nc.vector.tensor_tensor(
-                            out=added[bt][:, 0, :], in0=added[bt][:, 1, :], in1=cell_in[:], op=MULT
-                        )
-                        nc.vector.tensor_tensor(
-                            out=carried[bt][:], in0=carried[bt][:], in1=added[bt][:], op=ADD
-                        )
-                        rows = slice(P * bt, P * (bt + 1))
-                        nc.sync.dma_start(out=out_0[rows, cols], in_=carried[bt][:, 0, :])
-                        nc.sync.dma_start(out=out_1[rows, cols], in_=carried[bt][:, 1, :])
+                        new_c = work.tile([P, N_CHUNK], F32, name="new_c")
+                        new_n = work.tile([P, N_CHUNK], F32, name="new_n")
+                        for row, product in enumerate((new_c, new_n)):
+                            old = psum.tile([P, N_CHUNK], F32, name="old", tag="aux", bufs=4)
+                            nc.tensor.matmul(
+                                out=old[:], lhsT=ident_bf[:], rhs=prev[nch][:, bt, row, :], start=True, stop=True
+                            )
+                            nc.vector.tensor_tensor(out=product[:], in0=forget[:], in1=old[:], op=MULT)
+                        nc.gpsimd.tensor_tensor(out=new_c[:], in0=new_c[:], in1=fresh[bt][:], op=ADD)
+                        nc.vector.tensor_tensor(out=new_n[:], in0=new_n[:], in1=in_gate[bt][:], op=ADD)
+                        nc.sync.dma_start(out=out_0[rows, cols], in_=new_c[:])
+                        nc.sync.dma_start(out=out_1[rows, cols], in_=new_n[:])

@@ -53,7 +53,7 @@ def tile_slstmcell_pa_kernel(
         ident_bf = keep.tile([P, P], BF16, name="ident_bf")
         ones = keep.tile([P, P], BF16, name="ones")
         bias_rows = keep.tile([P, len(GATES), D_H], BF16, name="bias_rows")
-        raw = [keep.tile([P, 2, D_IN], BF16, name="raw%d" % bt) for bt in range(B_TILES)]
+        raw = [keep.tile([P, 2, 2, D_IN], BF16, name="raw%d" % pair) for pair in range(B_TILES // 2)]
         act_codes = keep.tile([P, B_TILES, PASSES * P], U32, name="act_codes", align_bytes=64)
         act_scales = keep.tile([P, B_TILES, PASSES * P], U8, name="act_scales", align_bytes=64)
         w_codes = {}
@@ -77,14 +77,13 @@ def tile_slstmcell_pa_kernel(
                 out=bias_rows[0:1, gi, :], in_=bias_of[gate].rearrange("(o n) -> o n", o=1)
             )
 
-        def load_planes(gate):
-            for s in range(2):
-                for quad in range(4):
-                    first = 32 * quad + 4 * HALVES * s
-                    nc.sync.dma_start(
-                        out=w_planes[gate][first : first + 4 * HALVES, :].bitcast(I32),
-                        in_=scales_of[gate][s][:, 4 * quad : 4 * quad + 4, :].bitcast(I32),
-                    )
+        def load_planes(gate, s):
+            for quad in range(4):
+                first = 32 * quad + 4 * HALVES * s
+                nc.sync.dma_start(
+                    out=w_planes[gate][first : first + 4 * HALVES, :].bitcast(I32),
+                    in_=scales_of[gate][s][:, 4 * quad : 4 * quad + 4, :].bitcast(I32),
+                )
 
         def load_words(gate, nch):
             for s in range(2):
@@ -102,11 +101,18 @@ def tile_slstmcell_pa_kernel(
                     in_=source.rearrange("(bt p) n -> p bt n", p=P)[:, :, cols],
                 )
 
-        for bt in range(B_TILES):
+        load_planes(GATES[0], 0)
+        for pair in range(B_TILES // 2):
             for s, source in enumerate((x, h_prev)):
-                nc.sync.dma_start(out=raw[bt][:, s, :], in_=source[P * bt : P * (bt + 1), :])
-        for gate in GATES:
-            load_planes(gate)
+                nc.sync.dma_start(
+                    out=raw[pair][:, s, :, :],
+                    in_=source[2 * P * pair : 2 * P * (pair + 1), :].rearrange("(bt p) k -> p bt k", p=P),
+                )
+        load_planes(GATES[0], 1)
+        load_words(GATES[0], 0)
+        for gate in GATES[1:]:
+            load_planes(gate, 0)
+            load_planes(gate, 1)
             load_words(gate, 0)
         load_prev(0)
         for gate in GATES:
@@ -115,7 +121,7 @@ def tile_slstmcell_pa_kernel(
 
         for bt in range(B_TILES):
             for s in range(2):
-                pairs = raw[bt][:, s, :].bitcast(F32)
+                pairs = raw[bt // 2][:, s, bt % 2, :].bitcast(F32)
                 turned = psum.tile([P, HALVES * 2, P], F32, name="turned", tag="aux", bufs=4)
                 for g in range(HALVES):
                     for u in range(2):

@@ -24,7 +24,9 @@ PASSES = 2 * HALVES
 B_TILES = BATCH // P
 N_CHUNK = 512
 N_CHUNKS = D_H // N_CHUNK
-GATES = ("i", "z", "f")
+GATES = ("f", "i", "z")
+ACC_BANKS = 5
+AUX_BANKS = 3
 
 FLOPS = 2 * BATCH * (2 * D_IN) * (3 * D_H)
 
@@ -46,36 +48,58 @@ def tile_slstmcell_pa_kernel(
         keep = stack.enter_context(tc.tile_pool(name="keep", bufs=1))
         stage = stack.enter_context(tc.tile_pool(name="stage", bufs=4))
         work = stack.enter_context(tc.tile_pool(name="work", bufs=4))
-        state = stack.enter_context(tc.tile_pool(name="state", bufs=2 * B_TILES))
+        hold = stack.enter_context(tc.tile_pool(name="hold", bufs=2 * B_TILES))
         psum = stack.enter_context(tc.psum_pool(name="psum", bufs=1))
 
         ident = keep.tile([P, P], F32, name="ident")
         ident_bf = keep.tile([P, P], BF16, name="ident_bf")
         ones = keep.tile([P, P], BF16, name="ones")
+        warm = keep.tile([P, 1], F32, name="warm")
         bias_rows = keep.tile([P, len(GATES), D_H], BF16, name="bias_rows")
-        raw = [keep.tile([P, 2, 2, D_IN], BF16, name="raw%d" % pair) for pair in range(B_TILES // 2)]
-        act_codes = keep.tile([P, B_TILES, PASSES * P], U32, name="act_codes", align_bytes=64)
-        act_scales = keep.tile([P, B_TILES, PASSES * P], U8, name="act_scales", align_bytes=64)
+        raw = {}
+        act_codes = {}
+        act_scales = {}
+        for s in range(2):
+            for pair in range(B_TILES // 2):
+                raw[s, pair] = keep.tile([P, 2, D_IN], BF16, name="raw%d%d" % (s, pair))
+            for bt in range(B_TILES):
+                act_codes[s, bt] = keep.tile([P, HALVES * P], U32, name="ac%d%d" % (s, bt), align_bytes=64)
+                act_scales[s, bt] = keep.tile([P, HALVES * P], U8, name="as%d%d" % (s, bt), align_bytes=64)
         w_codes = {}
         for gate in GATES:
             for nch in range(N_CHUNKS):
-                w_codes[gate, nch] = keep.tile(
-                    [P, PASSES, N_CHUNK], U32, name="w_%s%d" % (gate, nch), align_bytes=64
-                )
+                for s in range(2):
+                    w_codes[gate, nch, s] = keep.tile(
+                        [P, HALVES, N_CHUNK], U32, name="w_%s%d%d" % (gate, nch, s), align_bytes=64
+                    )
         w_planes = {g: keep.tile([P, D_H], U8, name="planes_%s" % g, align_bytes=64) for g in GATES}
         bias = {g: keep.tile([P, D_H], BF16, name="bias_%s" % g) for g in GATES}
-        prev = [keep.tile([P, B_TILES, 2, N_CHUNK], BF16, name="prev%d" % nch) for nch in range(N_CHUNKS)]
+        prev_c = [keep.tile([P, B_TILES, N_CHUNK], BF16, name="prev_c%d" % nch) for nch in range(N_CHUNKS)]
+        prev_n = [keep.tile([P, B_TILES, N_CHUNK], BF16, name="prev_n%d" % nch) for nch in range(N_CHUNKS)]
 
-        for gate in GATES:
+        nc.vector.memset(w_planes[GATES[0]][:].bitcast(I32), 0)
+        nc.vector.memset(ones[:], 1.0)
+        nc.vector.memset(bias_rows[:].rearrange("p g n -> p (g n)").bitcast(I32), 0)
+        for gate in GATES[1:]:
             nc.vector.memset(w_planes[gate][:].bitcast(I32), 0)
         make_identity(nc, ident[:])
         make_identity(nc, ident_bf[:])
-        nc.vector.memset(ones[:], 1.0)
-        nc.vector.memset(bias_rows[:].rearrange("p g n -> p (g n)").bitcast(I32), 0)
+
+        stack.enter_context(tc.manual_schedule())
+
         for gi, gate in enumerate(GATES):
             nc.scalar.dma_start(
                 out=bias_rows[0:1, gi, :], in_=bias_of[gate].rearrange("(o n) -> o n", o=1)
             )
+        nc.scalar.activation(out=warm[:], in_=ones[:, 0:1], func=EXP)
+
+        def load_acts(s):
+            source = (x, h_prev)[s]
+            for pair in range(B_TILES // 2):
+                nc.sync.dma_start(
+                    out=raw[s, pair][:],
+                    in_=source[2 * P * pair : 2 * P * (pair + 1), :].rearrange("(bt p) k -> p bt k", p=P),
+                )
 
         def load_planes(gate, s):
             for quad in range(4):
@@ -85,109 +109,180 @@ def tile_slstmcell_pa_kernel(
                     in_=scales_of[gate][s][:, 4 * quad : 4 * quad + 4, :].bitcast(I32),
                 )
 
-        def load_words(gate, nch):
-            for s in range(2):
-                by_partition = words_of[gate][s].rearrange("g p n t -> p g (n t)")
-                nc.sync.dma_start(
-                    out=w_codes[gate, nch][:, HALVES * s : HALVES * (s + 1), :].bitcast(I32),
-                    in_=by_partition[:, :, 4 * N_CHUNK * nch : 4 * N_CHUNK * (nch + 1)].bitcast(I32),
-                )
+        def load_words(gate, nch, s):
+            by_partition = words_of[gate][s].rearrange("g p n t -> p g (n t)")
+            nc.sync.dma_start(
+                out=w_codes[gate, nch, s][:].bitcast(I32),
+                in_=by_partition[:, :, 4 * N_CHUNK * nch : 4 * N_CHUNK * (nch + 1)].bitcast(I32),
+            )
 
         def load_prev(nch):
             cols = slice(N_CHUNK * nch, N_CHUNK * (nch + 1))
-            for row, source in enumerate((c_prev, n_prev)):
+            for tile_, source in ((prev_c[nch], c_prev), (prev_n[nch], n_prev)):
                 nc.sync.dma_start(
-                    out=prev[nch][:, :, row, :],
-                    in_=source.rearrange("(bt p) n -> p bt n", p=P)[:, :, cols],
+                    out=tile_[:], in_=source.rearrange("(bt p) n -> p bt n", p=P)[:, :, cols]
                 )
 
-        load_planes(GATES[0], 0)
-        for pair in range(B_TILES // 2):
-            for s, source in enumerate((x, h_prev)):
-                nc.sync.dma_start(
-                    out=raw[pair][:, s, :, :],
-                    in_=source[2 * P * pair : 2 * P * (pair + 1), :].rearrange("(bt p) k -> p bt k", p=P),
-                )
-        load_planes(GATES[0], 1)
-        load_words(GATES[0], 0)
-        for gate in GATES[1:]:
+        load_acts(0)
+        load_planes("f", 0)
+        load_planes("f", 1)
+        load_words("f", 0, 0)
+        load_acts(1)
+        load_words("f", 0, 1)
+        load_prev(0)
+        for gate in ("i", "z"):
             load_planes(gate, 0)
             load_planes(gate, 1)
-            load_words(gate, 0)
-        load_prev(0)
-        for gate in GATES:
-            load_words(gate, 1)
+            load_words(gate, 0, 0)
+            load_words(gate, 0, 1)
+        load_words("f", 1, 0)
+        load_words("f", 1, 1)
         load_prev(1)
+        for gate in ("i", "z"):
+            load_words(gate, 1, 0)
+            load_words(gate, 1, 1)
 
-        for bt in range(B_TILES):
-            for s in range(2):
-                pairs = raw[bt // 2][:, s, bt % 2, :].bitcast(F32)
-                turned = psum.tile([P, HALVES * 2, P], F32, name="turned", tag="aux", bufs=4)
-                for g in range(HALVES):
-                    for u in range(2):
-                        nc.tensor.transpose(
-                            turned[:, 2 * g + u, :],
-                            pairs[:, 256 * g + u : 256 * (g + 1) : 2],
-                            ident[:],
-                        )
-                grouped = stage.tile([P, HALVES, P, 4], BF16, name="grouped", align_bytes=64)
-                nc.scalar.copy(
-                    out=grouped[:].bitcast(F32),
-                    in_=turned[:].rearrange("p (g u) b -> p g b u", u=2),
-                )
-                cols = slice(HALVES * P * s, HALVES * P * (s + 1))
-                nc.vector.quantize_mx(
-                    out=act_codes[:, bt, cols].bitcast(FP8X4),
-                    scales=act_scales[:, bt, cols],
-                    in_=grouped[:].rearrange("p g b t -> p (g b t)"),
-                )
+        sorted_of = {}
 
-        for gi, gate in enumerate(GATES):
+        def sort_words(s, bt):
+            pairs = raw[s, bt // 2][:, bt % 2, :].bitcast(F32)
+            sorted_of[s, bt] = stage.tile([P, HALVES * 2, P], F32, name="sorted_words")
+            nc.vector.tensor_copy(
+                out=sorted_of[s, bt][:].rearrange("p (g u) w -> p g u w", u=2),
+                in_=pairs.rearrange("p (g w u) -> p g u w", g=HALVES, u=2),
+            )
+
+        def turn(s, bt):
+            sorted_words = sorted_of[s, bt]
+            turned = psum.tile([P, HALVES * 2, P], F32, name="turned", tag="aux", bufs=AUX_BANKS)
+            for gu in range(HALVES * 2):
+                nc.tensor.transpose(turned[:, gu, :], sorted_words[:, gu, :], ident[:])
+            grouped = stage.tile([P, HALVES, P, 4], BF16, name="grouped", align_bytes=64)
+            nc.scalar.copy(
+                out=grouped[:].bitcast(F32),
+                in_=turned[:].rearrange("p (g u) b -> p g b u", u=2),
+            )
+            nc.vector.quantize_mx(
+                out=act_codes[s, bt][:].bitcast(FP8X4),
+                scales=act_scales[s, bt][:],
+                in_=grouped[:].rearrange("p g b t -> p (g b t)"),
+            )
+
+        def spread(gate):
+            gi = GATES.index(gate)
+            wide = psum.tile([P, D_H], BF16, name="wide", tag="acc", bufs=ACC_BANKS)
             for nch in range(N_CHUNKS):
                 cols = slice(N_CHUNK * nch, N_CHUNK * (nch + 1))
-                spread = psum.tile([P, N_CHUNK], F32, name="spread", tag="aux", bufs=4)
-                nc.tensor.matmul(out=spread[:], lhsT=ones[:], rhs=bias_rows[:, gi, cols], start=True, stop=True)
-                nc.vector.tensor_copy(out=bias[gate][:, cols], in_=spread[:])
+                nc.tensor.matmul(out=wide[:, cols], lhsT=ones[:], rhs=bias_rows[:, gi, cols], start=True, stop=True)
+            nc.scalar.copy(out=bias[gate][:], in_=wide[:])
 
-        for nch in range(N_CHUNKS):
+        def passes(gate, nch, bt, acc, which):
             cols = slice(N_CHUNK * nch, N_CHUNK * (nch + 1))
-            in_gate = [None] * B_TILES
-            fresh = [None] * B_TILES
-            for gate in GATES:
-                for bt in range(B_TILES):
-                    rows = slice(P * bt, P * (bt + 1))
-                    acc = psum.tile([P, N_CHUNK], F32, name="acc", tag="acc", bufs=4)
-                    for c in range(PASSES):
-                        nc.tensor.matmul_mx(
-                            out=acc[:],
-                            lhsT=act_codes[:, bt, P * c : P * (c + 1)].bitcast(FP8X4),
-                            lhsT_scale=act_scales[:, bt, P * c : P * (c + 1)],
-                            rhs=w_codes[gate, nch][:, c, :].bitcast(FP8X4),
-                            rhs_scale=w_planes[gate][4 * c : P, cols],
-                            start=(c == 0),
-                            stop=(c == PASSES - 1),
-                        )
-                    pre = work.tile([P, N_CHUNK], F32, name="pre")
-                    nc.vector.tensor_tensor(out=pre[:], in0=acc[:], in1=bias[gate][:, cols], op=ADD)
-                    if gate == "i":
-                        in_gate[bt] = state.tile([P, N_CHUNK], F32, name="in_gate")
-                        nc.scalar.activation(out=in_gate[bt][:], in_=pre[:], func=EXP)
-                    elif gate == "z":
-                        fresh[bt] = state.tile([P, N_CHUNK], F32, name="fresh")
-                        nc.scalar.activation(out=fresh[bt][:], in_=pre[:], func=TANH)
-                        nc.gpsimd.tensor_tensor(out=fresh[bt][:], in0=fresh[bt][:], in1=in_gate[bt][:], op=MULT)
+            for c in which:
+                s, g = divmod(c, HALVES)
+                nc.tensor.matmul_mx(
+                    out=acc[:],
+                    lhsT=act_codes[s, bt][:, P * g : P * (g + 1)].bitcast(FP8X4),
+                    lhsT_scale=act_scales[s, bt][:, P * g : P * (g + 1)],
+                    rhs=w_codes[gate, nch, s][:, g, :].bitcast(FP8X4),
+                    rhs_scale=w_planes[gate][4 * c : P, cols],
+                    start=(c == 0),
+                    stop=(c == PASSES - 1),
+                )
+
+        open_acc = {}
+        for bt in range(B_TILES):
+            sort_words(0, bt)
+        for bt in range(B_TILES):
+            turn(0, bt)
+        for bt in range(B_TILES):
+            sort_words(1, bt)
+        for bt in range(B_TILES):
+            open_acc[bt] = psum.tile([P, N_CHUNK], F32, name="acc", tag="acc", bufs=ACC_BANKS)
+            passes("f", 0, bt, open_acc[bt], (0, 1))
+        for bt in range(B_TILES):
+            turn(1, bt)
+        spread("f")
+
+        order = []
+        for nch in range(N_CHUNKS):
+            order.extend([("f", nch, bt) for bt in range(B_TILES)])
+            for bt in range(B_TILES):
+                order.extend((("i", nch, bt), ("z", nch, bt)))
+        last = len(order) - 1
+        later = {}
+        kept_c = {}
+        kept_n = {}
+        in_gate = {}
+
+        def f_products(nch, bt, forget, old):
+            def emit():
+                kept_c[nch, bt] = hold.tile([P, N_CHUNK], F32, name="kept_c")
+                kept_n[nch, bt] = hold.tile([P, N_CHUNK], F32, name="kept_n")
+                nc.vector.tensor_tensor(out=kept_c[nch, bt][:], in0=forget[:], in1=old[:], op=MULT)
+                nc.gpsimd.tensor_tensor(out=kept_n[nch, bt][:], in0=forget[:], in1=prev_n[nch][:, bt, :], op=MULT)
+            return emit
+
+        def finish_n(nch, bt):
+            def emit():
+                new_n = kept_n[nch, bt]
+                nc.vector.tensor_tensor(out=new_n[:], in0=new_n[:], in1=in_gate[nch, bt][:], op=ADD)
+                nc.sync.dma_start(
+                    out=out_1[P * bt : P * (bt + 1), N_CHUNK * nch : N_CHUNK * (nch + 1)], in_=new_n[:]
+                )
+            return emit
+
+        def fresh_product(engine, nch, bt, fresh):
+            def emit():
+                engine.tensor_tensor(out=fresh[:], in0=fresh[:], in1=in_gate[nch, bt][:], op=MULT)
+            return emit
+
+        def finish_c(engine, nch, bt, fresh):
+            def emit():
+                new_c = kept_c[nch, bt]
+                engine.tensor_tensor(out=new_c[:], in0=new_c[:], in1=fresh[:], op=ADD)
+                nc.sync.dma_start(
+                    out=out_0[P * bt : P * (bt + 1), N_CHUNK * nch : N_CHUNK * (nch + 1)], in_=new_c[:]
+                )
+            return emit
+
+        for slot in range(len(order) + 4):
+            if slot <= last:
+                gate, nch, bt = order[slot]
+                cols = slice(N_CHUNK * nch, N_CHUNK * (nch + 1))
+                if gate == "f" and nch == 0:
+                    acc = open_acc[bt]
+                    passes(gate, nch, bt, acc, (2, 3))
+                else:
+                    acc = psum.tile([P, N_CHUNK], F32, name="acc", tag="acc", bufs=ACC_BANKS)
+                    passes(gate, nch, bt, acc, range(PASSES))
+                pre = work.tile([P, N_CHUNK], F32, name="pre")
+                nc.vector.tensor_tensor(out=pre[:], in0=acc[:], in1=bias[gate][:, cols], op=ADD)
+                if gate == "f":
+                    old = psum.tile([P, N_CHUNK], F32, name="old", tag="aux", bufs=AUX_BANKS)
+                    nc.tensor.matmul(out=old[:], lhsT=ident_bf[:], rhs=prev_c[nch][:, bt, :], start=True, stop=True)
+                    forget = work.tile([P, N_CHUNK], F32, name="forget")
+                    nc.scalar.activation(out=forget[:], in_=pre[:], func=EXP)
+                    later.setdefault(slot + 1, []).append(f_products(nch, bt, forget, old))
+                elif gate == "i":
+                    in_gate[nch, bt] = work.tile([P, N_CHUNK], F32, name="in_gate")
+                    nc.scalar.activation(out=in_gate[nch, bt][:], in_=pre[:], func=EXP)
+                    later.setdefault(slot + 1, []).append(finish_n(nch, bt))
+                else:
+                    fresh = work.tile([P, N_CHUNK], F32, name="fresh")
+                    nc.scalar.activation(out=fresh[:], in_=pre[:], func=TANH)
+                    if slot == last:
+                        later.setdefault(slot + 1, []).append(fresh_product(nc.vector, nch, bt, fresh))
+                        later.setdefault(slot + 1, []).append(finish_c(nc.vector, nch, bt, fresh))
                     else:
-                        forget = work.tile([P, N_CHUNK], F32, name="forget")
-                        nc.scalar.activation(out=forget[:], in_=pre[:], func=EXP)
-                        new_c = work.tile([P, N_CHUNK], F32, name="new_c")
-                        new_n = work.tile([P, N_CHUNK], F32, name="new_n")
-                        for row, product in enumerate((new_c, new_n)):
-                            old = psum.tile([P, N_CHUNK], F32, name="old", tag="aux", bufs=4)
-                            nc.tensor.matmul(
-                                out=old[:], lhsT=ident_bf[:], rhs=prev[nch][:, bt, row, :], start=True, stop=True
-                            )
-                            nc.vector.tensor_tensor(out=product[:], in0=forget[:], in1=old[:], op=MULT)
-                        nc.gpsimd.tensor_tensor(out=new_c[:], in0=new_c[:], in1=fresh[bt][:], op=ADD)
-                        nc.vector.tensor_tensor(out=new_n[:], in0=new_n[:], in1=in_gate[bt][:], op=ADD)
-                        nc.sync.dma_start(out=out_0[rows, cols], in_=new_c[:])
-                        nc.sync.dma_start(out=out_1[rows, cols], in_=new_n[:])
+                        later.setdefault(slot + 1, []).append(fresh_product(nc.gpsimd, nch, bt, fresh))
+                        if bt % 2 == 0:
+                            later.setdefault(slot + 1, []).append(finish_c(nc.gpsimd, nch, bt, fresh))
+                        else:
+                            later.setdefault(slot + 3, []).append(finish_c(nc.vector, nch, bt, fresh))
+                if slot == 1:
+                    spread("i")
+                if slot == 2:
+                    spread("z")
+            for emit in later.get(slot, []):
+                emit()

@@ -72,16 +72,16 @@ def tile_slstmcell_pa_kernel(
                     w_codes[gate, nch, s] = keep.tile(
                         [P, HALVES, N_CHUNK], U32, name="w_%s%d%d" % (gate, nch, s), align_bytes=64
                     )
-        w_planes = {g: keep.tile([P, D_H], U8, name="planes_%s" % g, align_bytes=64) for g in GATES}
+        w_planes = {g: keep.tile([P, 2, D_H], U8, name="planes_%s" % g, align_bytes=64) for g in GATES}
         bias = {g: keep.tile([P, D_H], BF16, name="bias_%s" % g) for g in GATES}
         prev_c = [keep.tile([P, B_TILES, N_CHUNK], BF16, name="prev_c%d" % nch) for nch in range(N_CHUNKS)]
         prev_n = [keep.tile([P, B_TILES, N_CHUNK], BF16, name="prev_n%d" % nch) for nch in range(N_CHUNKS)]
 
-        nc.vector.memset(w_planes[GATES[0]][:].bitcast(I32), 0)
+        nc.vector.memset(w_planes[GATES[0]][:].rearrange("p s n -> p (s n)").bitcast(I32), 0)
         nc.vector.memset(ones[:], 1.0)
         nc.vector.memset(bias_rows[:].rearrange("p g n -> p (g n)").bitcast(I32), 0)
         for gate in GATES[1:]:
-            nc.vector.memset(w_planes[gate][:].bitcast(I32), 0)
+            nc.vector.memset(w_planes[gate][:].rearrange("p s n -> p (s n)").bitcast(I32), 0)
         make_identity(nc, ident[:])
         make_identity(nc, ident_bf[:])
 
@@ -93,19 +93,17 @@ def tile_slstmcell_pa_kernel(
             )
         nc.scalar.activation(out=warm[:], in_=ones[:, 0:1], func=EXP)
 
-        def load_acts(s):
+        def load_acts(s, pair):
             source = (x, h_prev)[s]
-            for pair in range(B_TILES // 2):
-                nc.sync.dma_start(
-                    out=raw[s, pair][:],
-                    in_=source[2 * P * pair : 2 * P * (pair + 1), :].rearrange("(bt p) k -> p bt k", p=P),
-                )
+            nc.sync.dma_start(
+                out=raw[s, pair][:],
+                in_=source[2 * P * pair : 2 * P * (pair + 1), :].rearrange("(bt p) k -> p bt k", p=P),
+            )
 
-        def load_planes(gate, s):
-            for quad in range(4):
-                first = 32 * quad + 4 * HALVES * s
+        def load_planes(gate, s, quads):
+            for quad in quads:
                 nc.sync.dma_start(
-                    out=w_planes[gate][first : first + 4 * HALVES, :].bitcast(I32),
+                    out=w_planes[gate][32 * quad : 32 * quad + 4 * HALVES, s, :].bitcast(I32),
                     in_=scales_of[gate][s][:, 4 * quad : 4 * quad + 4, :].bitcast(I32),
                 )
 
@@ -116,28 +114,37 @@ def tile_slstmcell_pa_kernel(
                 in_=by_partition[:, :, 4 * N_CHUNK * nch : 4 * N_CHUNK * (nch + 1)].bitcast(I32),
             )
 
-        def load_prev(nch):
+        def load_prev(tile_, source, nch):
             cols = slice(N_CHUNK * nch, N_CHUNK * (nch + 1))
-            for tile_, source in ((prev_c[nch], c_prev), (prev_n[nch], n_prev)):
-                nc.sync.dma_start(
-                    out=tile_[:], in_=source.rearrange("(bt p) n -> p bt n", p=P)[:, :, cols]
-                )
+            nc.sync.dma_start(out=tile_[:], in_=source.rearrange("(bt p) n -> p bt n", p=P)[:, :, cols])
 
-        load_acts(0)
-        load_planes("f", 0)
-        load_planes("f", 1)
+        load_acts(0, 0)
+        load_planes("f", 0, (0, 1, 2, 3))
+        load_acts(0, 1)
+        load_planes("f", 1, (0, 1))
         load_words("f", 0, 0)
-        load_acts(1)
+        load_planes("f", 1, (2, 3))
+        load_acts(1, 0)
+        load_planes("i", 0, (0, 1))
+        load_acts(1, 1)
+        load_planes("i", 0, (2, 3))
         load_words("f", 0, 1)
-        load_prev(0)
-        for gate in ("i", "z"):
-            load_planes(gate, 0)
-            load_planes(gate, 1)
-            load_words(gate, 0, 0)
-            load_words(gate, 0, 1)
+        load_planes("i", 1, (0, 1))
+        load_prev(prev_c[0], c_prev, 0)
+        load_planes("i", 1, (2, 3))
+        load_prev(prev_n[0], n_prev, 0)
+        load_planes("z", 0, (0, 1))
+        load_words("i", 0, 0)
+        load_planes("z", 0, (2, 3))
+        load_words("i", 0, 1)
+        load_planes("z", 1, (0, 1))
+        load_words("z", 0, 0)
+        load_planes("z", 1, (2, 3))
+        load_words("z", 0, 1)
         load_words("f", 1, 0)
         load_words("f", 1, 1)
-        load_prev(1)
+        load_prev(prev_c[1], c_prev, 1)
+        load_prev(prev_n[1], n_prev, 1)
         for gate in ("i", "z"):
             load_words(gate, 1, 0)
             load_words(gate, 1, 1)
@@ -185,7 +192,7 @@ def tile_slstmcell_pa_kernel(
                     lhsT=act_codes[s, bt][:, P * g : P * (g + 1)].bitcast(FP8X4),
                     lhsT_scale=act_scales[s, bt][:, P * g : P * (g + 1)],
                     rhs=w_codes[gate, nch, s][:, g, :].bitcast(FP8X4),
-                    rhs_scale=w_planes[gate][4 * c : P, cols],
+                    rhs_scale=w_planes[gate][4 * g : P, s, cols],
                     start=(c == 0),
                     stop=(c == PASSES - 1),
                 )

@@ -27,6 +27,7 @@ N_CHUNKS = D_H // N_CHUNK
 GATES = ("f", "i", "z")
 ACC_BANKS = 5
 AUX_BANKS = 3
+C_LAG = 2
 
 FLOPS = 2 * BATCH * (2 * D_IN) * (3 * D_H)
 
@@ -283,10 +284,7 @@ def tile_slstmcell_pa_kernel(
                         later.setdefault(slot + 1, []).append(finish_c(nc.vector, nch, bt, fresh))
                     else:
                         later.setdefault(slot + 1, []).append(fresh_product(nc.gpsimd, nch, bt, fresh))
-                        if bt % 2 == 0:
-                            later.setdefault(slot + 1, []).append(finish_c(nc.gpsimd, nch, bt, fresh))
-                        else:
-                            later.setdefault(slot + 3, []).append(finish_c(nc.vector, nch, bt, fresh))
+                        later.setdefault(slot + C_LAG, []).append(finish_c(nc.vector, nch, bt, fresh))
                 if slot == 1:
                     spread("i")
                 if slot == 2:

@@ -27,7 +27,38 @@ N_CHUNKS = D_H // N_CHUNK
 GATES = ("f", "i", "z")
 ACC_BANKS = 5
 AUX_BANKS = 3
-C_LAG = 2
+C_LAG = (3, 2)
+N_LAG = (1, 1)
+
+def make_loads():
+    loads = [("acts", 0, 0), ("planes", "f", 0, (0, 1)), ("acts", 1, 0), ("planes", "f", 0, (2, 3)),
+             ("acts", 0, 1), ("planes", "f", 1, (0, 1)), ("acts", 1, 1), ("planes", "f", 1, (2, 3)),
+             ("words", "f", 0, 0), ("planes", "i", 0, (0, 1)), ("words", "f", 0, 1), ("planes", "i", 0, (2, 3)),
+             ("c", 0), ("planes", "i", 1, (0, 1)), ("n", 0), ("planes", "i", 1, (2, 3)),
+             ("words", "i", 0, 0), ("planes", "z", 0, (0, 1)), ("words", "i", 0, 1), ("planes", "z", 0, (2, 3)),
+             ("words", "z", 0, 0), ("planes", "z", 1, (0, 1)), ("words", "z", 0, 1), ("planes", "z", 1, (2, 3)),
+             ("words", "f", 1, 0), ("words", "f", 1, 1), ("c", 1), ("n", 1),
+             ("words", "i", 1, 0), ("words", "i", 1, 1), ("words", "z", 1, 0), ("words", "z", 1, 1)]
+    return loads
+
+
+def make_plan():
+    plan = [("sort", 0, 0), ("sort", 0, 1), ("sort", 1, 0), ("sort", 1, 1)]
+    plan.extend([("turn", 0, 0), ("turn", 0, 1), ("turn", 1, 0), ("turn", 1, 1)])
+    plan.extend([("quant", 0, 0), ("sort", 0, 2), ("sort", 0, 3), ("quant", 0, 1), ("quant", 1, 0), ("quant", 1, 1)])
+    plan.extend([("spread", "f"), ("turn", 0, 2), ("turn", 0, 3), ("bias", "f")])
+    plan.extend([("sort", 1, 2), ("sort", 1, 3), ("spread", "i"), ("turn", 1, 2), ("turn", 1, 3), ("spread", "z")])
+    plan.extend([("quant", 0, 2), ("quant", 0, 3), ("quant", 1, 2), ("quant", 1, 3), ("bias", "i"), ("bias", "z")])
+    for bt in range(B_TILES):
+        plan.extend([("slot", "f", 0, bt), ("old", 0, bt)])
+    plan.extend([("slot", "i", 0, bt) for bt in range(B_TILES)])
+    plan.extend([("slot", "z", 0, bt) for bt in range(B_TILES)])
+    for bt in range(B_TILES):
+        plan.extend([("slot", "f", 1, bt), ("old", 1, bt)])
+    for bt in range(B_TILES):
+        plan.extend([("slot", "i", 1, bt), ("slot", "z", 1, bt)])
+    return plan
+
 
 FLOPS = 2 * BATCH * (2 * D_IN) * (3 * D_H)
 
@@ -119,38 +150,20 @@ def tile_slstmcell_pa_kernel(
             cols = slice(N_CHUNK * nch, N_CHUNK * (nch + 1))
             nc.sync.dma_start(out=tile_[:], in_=source.rearrange("(bt p) n -> p bt n", p=P)[:, :, cols])
 
-        load_acts(0, 0)
-        load_planes("f", 0, (0, 1, 2, 3))
-        load_acts(0, 1)
-        load_planes("f", 1, (0, 1))
-        load_words("f", 0, 0)
-        load_planes("f", 1, (2, 3))
-        load_acts(1, 0)
-        load_planes("i", 0, (0, 1))
-        load_acts(1, 1)
-        load_planes("i", 0, (2, 3))
-        load_words("f", 0, 1)
-        load_planes("i", 1, (0, 1))
-        load_prev(prev_c[0], c_prev, 0)
-        load_planes("i", 1, (2, 3))
-        load_prev(prev_n[0], n_prev, 0)
-        load_planes("z", 0, (0, 1))
-        load_words("i", 0, 0)
-        load_planes("z", 0, (2, 3))
-        load_words("i", 0, 1)
-        load_planes("z", 1, (0, 1))
-        load_words("z", 0, 0)
-        load_planes("z", 1, (2, 3))
-        load_words("z", 0, 1)
-        load_words("f", 1, 0)
-        load_words("f", 1, 1)
-        load_prev(prev_c[1], c_prev, 1)
-        load_prev(prev_n[1], n_prev, 1)
-        for gate in ("i", "z"):
-            load_words(gate, 1, 0)
-            load_words(gate, 1, 1)
+        for step in make_loads():
+            if step[0] == "acts":
+                load_acts(step[1], step[2])
+            elif step[0] == "planes":
+                load_planes(step[1], step[2], step[3])
+            elif step[0] == "words":
+                load_words(step[1], step[2], step[3])
+            elif step[0] == "c":
+                load_prev(prev_c[step[1]], c_prev, step[1])
+            else:
+                load_prev(prev_n[step[1]], n_prev, step[1])
 
         sorted_of = {}
+        grouped_of = {}
 
         def sort_words(s, bt):
             pairs = raw[s, bt // 2][:, bt % 2, :].bitcast(F32)
@@ -170,19 +183,26 @@ def tile_slstmcell_pa_kernel(
                 out=grouped[:].bitcast(F32),
                 in_=turned[:].rearrange("p (g u) b -> p g b u", u=2),
             )
+            grouped_of[s, bt] = grouped
+
+        def quantise(s, bt):
             nc.vector.quantize_mx(
                 out=act_codes[s, bt][:].bitcast(FP8X4),
                 scales=act_scales[s, bt][:],
-                in_=grouped[:].rearrange("p g b t -> p (g b t)"),
+                in_=grouped_of[s, bt][:].rearrange("p g b t -> p (g b t)"),
             )
+
+        wide = {}
 
         def spread(gate):
             gi = GATES.index(gate)
-            wide = psum.tile([P, D_H], BF16, name="wide", tag="acc", bufs=ACC_BANKS)
+            wide[gate] = psum.tile([P, D_H], BF16, name="wide", tag="acc", bufs=ACC_BANKS)
             for nch in range(N_CHUNKS):
                 cols = slice(N_CHUNK * nch, N_CHUNK * (nch + 1))
-                nc.tensor.matmul(out=wide[:, cols], lhsT=ones[:], rhs=bias_rows[:, gi, cols], start=True, stop=True)
-            nc.scalar.copy(out=bias[gate][:], in_=wide[:])
+                nc.tensor.matmul(out=wide[gate][:, cols], lhsT=ones[:], rhs=bias_rows[:, gi, cols], start=True, stop=True)
+
+        def keep_bias(gate):
+            nc.scalar.copy(out=bias[gate][:], in_=wide[gate][:])
 
         def passes(gate, nch, bt, acc, which):
             cols = slice(N_CHUNK * nch, N_CHUNK * (nch + 1))
@@ -198,37 +218,24 @@ def tile_slstmcell_pa_kernel(
                     stop=(c == PASSES - 1),
                 )
 
-        open_acc = {}
-        for bt in range(B_TILES):
-            sort_words(0, bt)
-        for bt in range(B_TILES):
-            turn(0, bt)
-        for bt in range(B_TILES):
-            sort_words(1, bt)
-        for bt in range(B_TILES):
-            open_acc[bt] = psum.tile([P, N_CHUNK], F32, name="acc", tag="acc", bufs=ACC_BANKS)
-            passes("f", 0, bt, open_acc[bt], (0, 1))
-        for bt in range(B_TILES):
-            turn(1, bt)
-        spread("f")
-
-        order = []
-        for nch in range(N_CHUNKS):
-            order.extend([("f", nch, bt) for bt in range(B_TILES)])
-            for bt in range(B_TILES):
-                order.extend((("i", nch, bt), ("z", nch, bt)))
-        last = len(order) - 1
         later = {}
         kept_c = {}
         kept_n = {}
         in_gate = {}
+        forget_of = {}
+        old_of = {}
+        plan = make_plan()
+        slots = [step for step in plan if step[0] == "slot"]
+        last = len(slots) - 1
 
-        def f_products(nch, bt, forget, old):
+        def f_products(nch, bt):
             def emit():
                 kept_c[nch, bt] = hold.tile([P, N_CHUNK], F32, name="kept_c")
                 kept_n[nch, bt] = hold.tile([P, N_CHUNK], F32, name="kept_n")
-                nc.vector.tensor_tensor(out=kept_c[nch, bt][:], in0=forget[:], in1=old[:], op=MULT)
-                nc.gpsimd.tensor_tensor(out=kept_n[nch, bt][:], in0=forget[:], in1=prev_n[nch][:, bt, :], op=MULT)
+                nc.vector.tensor_tensor(out=kept_c[nch, bt][:], in0=forget_of[nch, bt][:], in1=old_of[nch, bt][:], op=MULT)
+                nc.gpsimd.tensor_tensor(
+                    out=kept_n[nch, bt][:], in0=forget_of[nch, bt][:], in1=prev_n[nch][:, bt, :], op=MULT
+                )
             return emit
 
         def finish_n(nch, bt):
@@ -254,28 +261,42 @@ def tile_slstmcell_pa_kernel(
                 )
             return emit
 
-        for slot in range(len(order) + 4):
-            if slot <= last:
-                gate, nch, bt = order[slot]
+        def lay_old(nch, bt):
+            old_of[nch, bt] = psum.tile([P, N_CHUNK], F32, name="old", tag="aux", bufs=AUX_BANKS)
+            nc.tensor.matmul(
+                out=old_of[nch, bt][:], lhsT=ident_bf[:], rhs=prev_c[nch][:, bt, :], start=True, stop=True
+            )
+
+        slot = -1
+        for step in plan:
+            if step[0] == "sort":
+                sort_words(step[1], step[2])
+            elif step[0] == "turn":
+                turn(step[1], step[2])
+            elif step[0] == "quant":
+                quantise(step[1], step[2])
+            elif step[0] == "spread":
+                spread(step[1])
+            elif step[0] == "bias":
+                keep_bias(step[1])
+            elif step[0] == "old":
+                lay_old(step[1], step[2])
+                later.setdefault(slot + 1, []).append(f_products(step[1], step[2]))
+            else:
+                slot += 1
+                gate, nch, bt = step[1], step[2], step[3]
                 cols = slice(N_CHUNK * nch, N_CHUNK * (nch + 1))
-                if gate == "f" and nch == 0:
-                    acc = open_acc[bt]
-                    passes(gate, nch, bt, acc, (2, 3))
-                else:
-                    acc = psum.tile([P, N_CHUNK], F32, name="acc", tag="acc", bufs=ACC_BANKS)
-                    passes(gate, nch, bt, acc, range(PASSES))
+                acc = psum.tile([P, N_CHUNK], F32, name="acc", tag="acc", bufs=ACC_BANKS)
+                passes(gate, nch, bt, acc, range(PASSES))
                 pre = work.tile([P, N_CHUNK], F32, name="pre")
                 nc.vector.tensor_tensor(out=pre[:], in0=acc[:], in1=bias[gate][:, cols], op=ADD)
                 if gate == "f":
-                    old = psum.tile([P, N_CHUNK], F32, name="old", tag="aux", bufs=AUX_BANKS)
-                    nc.tensor.matmul(out=old[:], lhsT=ident_bf[:], rhs=prev_c[nch][:, bt, :], start=True, stop=True)
-                    forget = work.tile([P, N_CHUNK], F32, name="forget")
-                    nc.scalar.activation(out=forget[:], in_=pre[:], func=EXP)
-                    later.setdefault(slot + 1, []).append(f_products(nch, bt, forget, old))
+                    forget_of[nch, bt] = work.tile([P, N_CHUNK], F32, name="forget")
+                    nc.scalar.activation(out=forget_of[nch, bt][:], in_=pre[:], func=EXP)
                 elif gate == "i":
                     in_gate[nch, bt] = work.tile([P, N_CHUNK], F32, name="in_gate")
                     nc.scalar.activation(out=in_gate[nch, bt][:], in_=pre[:], func=EXP)
-                    later.setdefault(slot + 1, []).append(finish_n(nch, bt))
+                    later.setdefault(slot + N_LAG[nch], []).append(finish_n(nch, bt))
                 else:
                     fresh = work.tile([P, N_CHUNK], F32, name="fresh")
                     nc.scalar.activation(out=fresh[:], in_=pre[:], func=TANH)
@@ -284,10 +305,9 @@ def tile_slstmcell_pa_kernel(
                         later.setdefault(slot + 1, []).append(finish_c(nc.vector, nch, bt, fresh))
                     else:
                         later.setdefault(slot + 1, []).append(fresh_product(nc.gpsimd, nch, bt, fresh))
-                        later.setdefault(slot + C_LAG, []).append(finish_c(nc.vector, nch, bt, fresh))
-                if slot == 1:
-                    spread("i")
-                if slot == 2:
-                    spread("z")
-            for emit in later.get(slot, []):
+                        later.setdefault(slot + C_LAG[nch], []).append(finish_c(nc.vector, nch, bt, fresh))
+                for emit in later.get(slot, []):
+                    emit()
+        for rest in range(last + 1, last + 5):
+            for emit in later.get(rest, []):
                 emit()

@@ -29,14 +29,17 @@ ACC_BANKS = 5
 AUX_BANKS = 3
 C_LAG = (3, 2)
 N_LAG = (1, 1)
+N_ON_POOL = ()
+Z_ON_VECTOR = ()
 
 def make_loads():
     loads = [("acts", 0, 0), ("planes", "f", 0, (0, 1)), ("acts", 1, 0), ("planes", "f", 0, (2, 3)),
              ("acts", 0, 1), ("planes", "f", 1, (0, 1)), ("acts", 1, 1), ("planes", "f", 1, (2, 3)),
-             ("words", "f", 0, 0), ("planes", "i", 0, (0, 1)), ("words", "f", 0, 1), ("planes", "i", 0, (2, 3)),
-             ("c", 0), ("planes", "i", 1, (0, 1)), ("n", 0), ("planes", "i", 1, (2, 3)),
-             ("words", "i", 0, 0), ("planes", "z", 0, (0, 1)), ("words", "i", 0, 1), ("planes", "z", 0, (2, 3)),
-             ("words", "z", 0, 0), ("planes", "z", 1, (0, 1)), ("words", "z", 0, 1), ("planes", "z", 1, (2, 3)),
+             ("words", "f", 0, 0), ("words", "f", 0, 1), ("c", 0), ("n", 0),
+             ("planes", "i", 0, (0, 1, 2, 3)), ("planes", "i", 1, (0, 1, 2, 3)),
+             ("words", "i", 0, 0), ("words", "i", 0, 1),
+             ("planes", "z", 0, (0, 1, 2, 3)), ("planes", "z", 1, (0, 1, 2, 3)),
+             ("words", "z", 0, 0), ("words", "z", 0, 1),
              ("words", "f", 1, 0), ("words", "f", 1, 1), ("c", 1), ("n", 1),
              ("words", "i", 1, 0), ("words", "i", 1, 1), ("words", "z", 1, 0), ("words", "z", 1, 1)]
     return loads
@@ -201,8 +204,11 @@ def tile_slstmcell_pa_kernel(
                 cols = slice(N_CHUNK * nch, N_CHUNK * (nch + 1))
                 nc.tensor.matmul(out=wide[gate][:, cols], lhsT=ones[:], rhs=bias_rows[:, gi, cols], start=True, stop=True)
 
-        def keep_bias(gate):
-            nc.scalar.copy(out=bias[gate][:], in_=wide[gate][:])
+        def keep_bias(gate, on_vector):
+            if on_vector:
+                nc.vector.tensor_copy(out=bias[gate][:], in_=wide[gate][:])
+            else:
+                nc.scalar.copy(out=bias[gate][:], in_=wide[gate][:])
 
         def passes(gate, nch, bt, acc, which):
             cols = slice(N_CHUNK * nch, N_CHUNK * (nch + 1))
@@ -241,7 +247,7 @@ def tile_slstmcell_pa_kernel(
         def finish_n(nch, bt):
             def emit():
                 new_n = kept_n[nch, bt]
-                nc.vector.tensor_tensor(out=new_n[:], in0=new_n[:], in1=in_gate[nch, bt][:], op=ADD)
+                (nc.gpsimd if (nch, bt) in N_ON_POOL else nc.vector).tensor_tensor(out=new_n[:], in0=new_n[:], in1=in_gate[nch, bt][:], op=ADD)
                 nc.sync.dma_start(
                     out=out_1[P * bt : P * (bt + 1), N_CHUNK * nch : N_CHUNK * (nch + 1)], in_=new_n[:]
                 )
@@ -268,6 +274,7 @@ def tile_slstmcell_pa_kernel(
             )
 
         slot = -1
+        open_acc = {}
         for step in plan:
             if step[0] == "sort":
                 sort_words(step[1], step[2])
@@ -278,7 +285,10 @@ def tile_slstmcell_pa_kernel(
             elif step[0] == "spread":
                 spread(step[1])
             elif step[0] == "bias":
-                keep_bias(step[1])
+                keep_bias(step[1], len(step) > 2)
+            elif step[0] == "xpart":
+                open_acc[step[1]] = psum.tile([P, N_CHUNK], F32, name="acc", tag="acc", bufs=ACC_BANKS)
+                passes("f", 0, step[1], open_acc[step[1]], (0, 1))
             elif step[0] == "old":
                 lay_old(step[1], step[2])
                 later.setdefault(slot + 1, []).append(f_products(step[1], step[2]))
@@ -286,8 +296,12 @@ def tile_slstmcell_pa_kernel(
                 slot += 1
                 gate, nch, bt = step[1], step[2], step[3]
                 cols = slice(N_CHUNK * nch, N_CHUNK * (nch + 1))
-                acc = psum.tile([P, N_CHUNK], F32, name="acc", tag="acc", bufs=ACC_BANKS)
-                passes(gate, nch, bt, acc, range(PASSES))
+                if gate == "f" and nch == 0 and bt in open_acc:
+                    acc = open_acc[bt]
+                    passes(gate, nch, bt, acc, (2, 3))
+                else:
+                    acc = psum.tile([P, N_CHUNK], F32, name="acc", tag="acc", bufs=ACC_BANKS)
+                    passes(gate, nch, bt, acc, range(PASSES))
                 pre = work.tile([P, N_CHUNK], F32, name="pre")
                 nc.vector.tensor_tensor(out=pre[:], in0=acc[:], in1=bias[gate][:, cols], op=ADD)
                 if gate == "f":
@@ -304,7 +318,7 @@ def tile_slstmcell_pa_kernel(
                         later.setdefault(slot + 1, []).append(fresh_product(nc.vector, nch, bt, fresh))
                         later.setdefault(slot + 1, []).append(finish_c(nc.vector, nch, bt, fresh))
                     else:
-                        later.setdefault(slot + 1, []).append(fresh_product(nc.gpsimd, nch, bt, fresh))
+                        later.setdefault(slot + 1, []).append(fresh_product(nc.vector if (nch, bt) in Z_ON_VECTOR else nc.gpsimd, nch, bt, fresh))
                         later.setdefault(slot + C_LAG[nch], []).append(finish_c(nc.vector, nch, bt, fresh))
                 for emit in later.get(slot, []):
                     emit()

@@ -33,28 +33,30 @@ N_ON_POOL = ()
 Z_ON_VECTOR = ()
 
 def make_loads():
-    loads = [("acts", 0, 0), ("planes", "f", 0, (0, 1)), ("acts", 1, 0), ("planes", "f", 0, (2, 3)),
-             ("acts", 0, 1), ("planes", "f", 1, (0, 1)), ("acts", 1, 1), ("planes", "f", 1, (2, 3)),
-             ("words", "f", 0, 0), ("words", "f", 0, 1), ("c", 0), ("n", 0),
-             ("planes", "i", 0, (0, 1, 2, 3)), ("planes", "i", 1, (0, 1, 2, 3)),
-             ("words", "i", 0, 0), ("words", "i", 0, 1),
-             ("planes", "z", 0, (0, 1, 2, 3)), ("planes", "z", 1, (0, 1, 2, 3)),
-             ("words", "z", 0, 0), ("words", "z", 0, 1),
-             ("words", "f", 1, 0), ("words", "f", 1, 1), ("c", 1), ("n", 1),
+    loads = [("act", 0, 0), ("biases", ("f", "i")), ("act", 0, 1), ("acts", 1, 0), ("planes", "f", 0, (0, 1)), ("acts", 0, 1), ("planes", "f", 0, (2, 3)),
+             ("acts", 1, 1), ("planes", "f", 1, (0, 1)), ("words", "f", 0, 0), ("planes", "f", 1, (2, 3)),
+             ("words", "f", 0, 1), ("planes", "i", 0, (0, 1)), ("c", 0), ("planes", "i", 0, (2, 3)),
+             ("n", 0), ("planes", "i", 1, (0, 1)), ("words", "i", 0, 0), ("planes", "i", 1, (2, 3)),
+             ("words", "i", 0, 1), ("planes", "z", 0, (0, 1)), ("words", "z", 0, 0), ("planes", "z", 0, (2, 3)),
+             ("planes", "z", 1, (0, 1)), ("words", "z", 0, 1), ("planes", "z", 1, (2, 3)),
+             ("wide_bias", "z"), ("words", "f", 1, 0), ("words", "f", 1, 1), ("c", 1), ("n", 1),
              ("words", "i", 1, 0), ("words", "i", 1, 1), ("words", "z", 1, 0), ("words", "z", 1, 1)]
     return loads
 
 
 def make_plan():
-    plan = [("sort", 0, 0), ("sort", 0, 1), ("sort", 1, 0), ("sort", 1, 1)]
-    plan.extend([("turn", 0, 0), ("turn", 0, 1), ("turn", 1, 0), ("turn", 1, 1)])
-    plan.extend([("quant", 0, 0), ("sort", 0, 2), ("sort", 0, 3), ("quant", 0, 1), ("quant", 1, 0), ("quant", 1, 1)])
-    plan.extend([("spread", "f"), ("turn", 0, 2), ("turn", 0, 3), ("bias", "f")])
-    plan.extend([("sort", 1, 2), ("sort", 1, 3), ("spread", "i"), ("turn", 1, 2), ("turn", 1, 3), ("spread", "z")])
-    plan.extend([("quant", 0, 2), ("quant", 0, 3), ("quant", 1, 2), ("quant", 1, 3), ("bias", "i"), ("bias", "z")])
+    plan = [("idle", 3)] if 3 else []
+    plan.extend([("turn", 0, 0), ("spread", "f"), ("bias", "f", "v"), ("turn", 0, 1), ("quant", 0, 0), ("spread", "i"), ("quant", 0, 1), ("bias", "i", "v")])
+    plan.extend([("turn", 1, 0), ("turn", 1, 1), ("quant", 1, 0), ("quant", 1, 1)])
+    plan.extend([("turn", 0, 2), ("turn", 0, 3), ("quant", 0, 2), ("quant", 0, 3)])
+    plan.extend([("turn", 1, 2), ("turn", 1, 3), ("quant", 1, 2), ("quant", 1, 3)])
+    plan.extend([("xpart", bt) for bt in range(2)])
     for bt in range(B_TILES):
-        plan.extend([("slot", "f", 0, bt), ("old", 0, bt)])
-    plan.extend([("slot", "i", 0, bt) for bt in range(B_TILES)])
+        plan.append(("slot", "f", 0, bt))
+        if bt > 0:
+            plan.append(("old", 0, bt - 1))
+    plan.extend([("slot", "i", 0, 0), ("old", 0, B_TILES - 1)])
+    plan.extend([("slot", "i", 0, bt) for bt in range(1, B_TILES)])
     plan.extend([("slot", "z", 0, bt) for bt in range(B_TILES)])
     for bt in range(B_TILES):
         plan.extend([("slot", "f", 1, bt), ("old", 1, bt)])
@@ -88,9 +90,9 @@ def tile_slstmcell_pa_kernel(
 
         ident = keep.tile([P, P], F32, name="ident")
         ident_bf = keep.tile([P, P], BF16, name="ident_bf")
-        ones = keep.tile([P, P], BF16, name="ones")
-        warm = keep.tile([P, 1], F32, name="warm")
-        bias_rows = keep.tile([P, len(GATES), D_H], BF16, name="bias_rows")
+        warm = keep.tile([P, 2], F32, name="warm")
+        zeros = keep.tile([P, N_CHUNK], BF16, name="zeros")
+        bias_rows = keep.tile([P, N_CHUNK], BF16, name="bias_rows")
         raw = {}
         act_codes = {}
         act_scales = {}
@@ -112,21 +114,18 @@ def tile_slstmcell_pa_kernel(
         prev_c = [keep.tile([P, B_TILES, N_CHUNK], BF16, name="prev_c%d" % nch) for nch in range(N_CHUNKS)]
         prev_n = [keep.tile([P, B_TILES, N_CHUNK], BF16, name="prev_n%d" % nch) for nch in range(N_CHUNKS)]
 
+        nc.vector.memset(bias_rows[:].bitcast(I32), 0)
+        nc.vector.memset(zeros[:].bitcast(I32), 0)
+        nc.vector.memset(warm[:, 0:1], 0.0)
         nc.vector.memset(w_planes[GATES[0]][:].rearrange("p s n -> p (s n)").bitcast(I32), 0)
-        nc.vector.memset(ones[:], 1.0)
-        nc.vector.memset(bias_rows[:].rearrange("p g n -> p (g n)").bitcast(I32), 0)
         for gate in GATES[1:]:
             nc.vector.memset(w_planes[gate][:].rearrange("p s n -> p (s n)").bitcast(I32), 0)
-        make_identity(nc, ident[:])
         make_identity(nc, ident_bf[:])
+        make_identity(nc, ident[:])
 
         stack.enter_context(tc.manual_schedule())
 
-        for gi, gate in enumerate(GATES):
-            nc.scalar.dma_start(
-                out=bias_rows[0:1, gi, :], in_=bias_of[gate].rearrange("(o n) -> o n", o=1)
-            )
-        nc.scalar.activation(out=warm[:], in_=ones[:, 0:1], func=EXP)
+        nc.scalar.activation(out=warm[:, 1:2], in_=warm[:, 0:1], func=EXP)
 
         def load_acts(s, pair):
             source = (x, h_prev)[s]
@@ -134,6 +133,22 @@ def tile_slstmcell_pa_kernel(
                 out=raw[s, pair][:],
                 in_=source[2 * P * pair : 2 * P * (pair + 1), :].rearrange("(bt p) k -> p bt k", p=P),
             )
+
+        def load_act_tile(s, bt):
+            nc.sync.dma_start(
+                out=raw[s, bt // 2][:, bt % 2, :], in_=(x, h_prev)[s][P * bt : P * (bt + 1), :]
+            )
+
+        def load_biases(gates):
+            for gate in gates:
+                gi = GATES.index(gate)
+                nc.sync.dma_start(
+                    out=bias_rows[N_CHUNKS * gi : N_CHUNKS * (gi + 1), :],
+                    in_=bias_of[gate].rearrange("(o n) -> o n", o=N_CHUNKS),
+                )
+
+        def load_wide_bias(gate):
+            nc.sync.dma_start(out=bias[gate][:], in_=bias_of[gate].partition_broadcast(P))
 
         def load_planes(gate, s, quads):
             for quad in quads:
@@ -156,6 +171,12 @@ def tile_slstmcell_pa_kernel(
         for step in make_loads():
             if step[0] == "acts":
                 load_acts(step[1], step[2])
+            elif step[0] == "act":
+                load_act_tile(step[1], step[2])
+            elif step[0] == "biases":
+                load_biases(step[1])
+            elif step[0] == "wide_bias":
+                load_wide_bias(step[1])
             elif step[0] == "planes":
                 load_planes(step[1], step[2], step[3])
             elif step[0] == "words":
@@ -177,10 +198,11 @@ def tile_slstmcell_pa_kernel(
             )
 
         def turn(s, bt):
-            sorted_words = sorted_of[s, bt]
+            words = raw[s, bt // 2][:, bt % 2, :].bitcast(F32)
             turned = psum.tile([P, HALVES * 2, P], F32, name="turned", tag="aux", bufs=AUX_BANKS)
             for gu in range(HALVES * 2):
-                nc.tensor.transpose(turned[:, gu, :], sorted_words[:, gu, :], ident[:])
+                g, u = divmod(gu, 2)
+                nc.tensor.transpose(turned[:, gu, :], words[:, 2 * P * g + u : 2 * P * (g + 1) : 2], ident[:])
             grouped = stage.tile([P, HALVES, P, 4], BF16, name="grouped", align_bytes=64)
             nc.scalar.copy(
                 out=grouped[:].bitcast(F32),
@@ -198,11 +220,21 @@ def tile_slstmcell_pa_kernel(
         wide = {}
 
         def spread(gate):
-            gi = GATES.index(gate)
             wide[gate] = psum.tile([P, D_H], BF16, name="wide", tag="acc", bufs=ACC_BANKS)
             for nch in range(N_CHUNKS):
                 cols = slice(N_CHUNK * nch, N_CHUNK * (nch + 1))
-                nc.tensor.matmul(out=wide[gate][:, cols], lhsT=ones[:], rhs=bias_rows[:, gi, cols], start=True, stop=True)
+                nc.tensor.matmul(
+                    out=wide[gate][:, cols],
+                    lhsT=ident_bf[:, N_CHUNKS * GATES.index(gate) + nch : N_CHUNKS * GATES.index(gate) + nch + 1].to_broadcast([P, P]),
+                    rhs=bias_rows[:],
+                    start=True,
+                    stop=True,
+                )
+
+        def idle(count):
+            scratch = psum.tile([P, N_CHUNK], F32, name="scratch", tag="acc", bufs=ACC_BANKS)
+            for turn_no in range(count):
+                nc.tensor.matmul(out=scratch[:], lhsT=zeros[:, 0:P], rhs=zeros[:], start=True, stop=True)
 
         def keep_bias(gate, on_vector):
             if on_vector:
@@ -238,7 +270,12 @@ def tile_slstmcell_pa_kernel(
             def emit():
                 kept_c[nch, bt] = hold.tile([P, N_CHUNK], F32, name="kept_c")
                 kept_n[nch, bt] = hold.tile([P, N_CHUNK], F32, name="kept_n")
-                nc.vector.tensor_tensor(out=kept_c[nch, bt][:], in0=forget_of[nch, bt][:], in1=old_of[nch, bt][:], op=MULT)
+                nc.vector.tensor_tensor(
+                    out=kept_c[nch, bt][:],
+                    in0=forget_of[nch, bt][:],
+                    in1=old_of[nch, bt][:] if (nch, bt) in old_of else prev_c[nch][:, bt, :],
+                    op=MULT,
+                )
                 nc.gpsimd.tensor_tensor(
                     out=kept_n[nch, bt][:], in0=forget_of[nch, bt][:], in1=prev_n[nch][:, bt, :], op=MULT
                 )
@@ -282,6 +319,8 @@ def tile_slstmcell_pa_kernel(
                 turn(step[1], step[2])
             elif step[0] == "quant":
                 quantise(step[1], step[2])
+            elif step[0] == "idle":
+                idle(step[1])
             elif step[0] == "spread":
                 spread(step[1])
             elif step[0] == "bias":
@@ -289,8 +328,9 @@ def tile_slstmcell_pa_kernel(
             elif step[0] == "xpart":
                 open_acc[step[1]] = psum.tile([P, N_CHUNK], F32, name="acc", tag="acc", bufs=ACC_BANKS)
                 passes("f", 0, step[1], open_acc[step[1]], (0, 1))
-            elif step[0] == "old":
-                lay_old(step[1], step[2])
+            elif step[0] in ("old", "plain"):
+                if step[0] == "old":
+                    lay_old(step[1], step[2])
                 later.setdefault(slot + 1, []).append(f_products(step[1], step[2]))
             else:
                 slot += 1

@@ -33,30 +33,27 @@ N_ON_POOL = ()
 Z_ON_VECTOR = ()
 
 def make_loads():
-    loads = [("act", 0, 0), ("biases", ("f", "i")), ("act", 0, 1), ("acts", 1, 0), ("planes", "f", 0, (0, 1)), ("acts", 0, 1), ("planes", "f", 0, (2, 3)),
+    loads = [("act", 0, 0), ("biases", GATES), ("act", 0, 1), ("acts", 1, 0), ("planes", "f", 0, (0, 1)), ("acts", 0, 1), ("planes", "f", 0, (2, 3)),
              ("acts", 1, 1), ("planes", "f", 1, (0, 1)), ("words", "f", 0, 0), ("planes", "f", 1, (2, 3)),
              ("words", "f", 0, 1), ("planes", "i", 0, (0, 1)), ("c", 0), ("planes", "i", 0, (2, 3)),
              ("n", 0), ("planes", "i", 1, (0, 1)), ("words", "i", 0, 0), ("planes", "i", 1, (2, 3)),
              ("words", "i", 0, 1), ("planes", "z", 0, (0, 1)), ("words", "z", 0, 0), ("planes", "z", 0, (2, 3)),
              ("planes", "z", 1, (0, 1)), ("words", "z", 0, 1), ("planes", "z", 1, (2, 3)),
-             ("wide_bias", "z"), ("words", "f", 1, 0), ("words", "f", 1, 1), ("c", 1), ("n", 1),
+             ("words", "f", 1, 0), ("words", "f", 1, 1), ("c", 1), ("n", 1),
              ("words", "i", 1, 0), ("words", "i", 1, 1), ("words", "z", 1, 0), ("words", "z", 1, 1)]
     return loads
 
 
 def make_plan():
     plan = [("idle", 3)] if 3 else []
-    plan.extend([("turn", 0, 0), ("spread", "f"), ("bias", "f", "v"), ("turn", 0, 1), ("quant", 0, 0), ("spread", "i"), ("quant", 0, 1), ("bias", "i", "v")])
-    plan.extend([("turn", 1, 0), ("turn", 1, 1), ("quant", 1, 0), ("quant", 1, 1)])
-    plan.extend([("turn", 0, 2), ("turn", 0, 3), ("quant", 0, 2), ("quant", 0, 3)])
+    plan.extend([("turn", 0, 0), ("spread", "f"), ("bias", "f", "v"), ("turn", 0, 1), ("quant", 0, 0), ("quant", 0, 1)])
+    plan.extend([("turn", 1, 0), ("turn", 1, 1), ("spread", "i"), ("quant", 1, 0), ("quant", 1, 1), ("bias", "i", "v")])
+    plan.extend([("turn", 0, 2), ("turn", 0, 3), ("spread", "z"), ("quant", 0, 2), ("quant", 0, 3), ("bias", "z", "v")])
     plan.extend([("turn", 1, 2), ("turn", 1, 3), ("quant", 1, 2), ("quant", 1, 3)])
-    plan.extend([("xpart", bt) for bt in range(2)])
+    plan.extend([("xpart", bt) for bt in range(0)])
     for bt in range(B_TILES):
-        plan.append(("slot", "f", 0, bt))
-        if bt > 0:
-            plan.append(("old", 0, bt - 1))
-    plan.extend([("slot", "i", 0, 0), ("old", 0, B_TILES - 1)])
-    plan.extend([("slot", "i", 0, bt) for bt in range(1, B_TILES)])
+        plan.extend([("slot", "f", 0, bt), ("old", 0, bt)])
+    plan.extend([("slot", "i", 0, bt) for bt in range(B_TILES)])
     plan.extend([("slot", "z", 0, bt) for bt in range(B_TILES)])
     for bt in range(B_TILES):
         plan.extend([("slot", "f", 1, bt), ("old", 1, bt)])

@@ -30,15 +30,14 @@ AUX_BANKS = 3
 C_LAG = (3, 2)
 N_LAG = (1, 1)
 N_ON_POOL = ()
+SPLIT_LAST = 1
 Z_ON_VECTOR = ()
 
 def make_loads():
     loads = [("act", 0, 0), ("biases", GATES), ("act", 0, 1), ("acts", 1, 0), ("planes", "f", 0, (0, 1)), ("acts", 0, 1), ("planes", "f", 0, (2, 3)),
              ("acts", 1, 1), ("planes", "f", 1, (0, 1)), ("words", "f", 0, 0), ("planes", "f", 1, (2, 3)),
-             ("words", "f", 0, 1), ("planes", "i", 0, (0, 1)), ("c", 0), ("planes", "i", 0, (2, 3)),
-             ("n", 0), ("planes", "i", 1, (0, 1)), ("words", "i", 0, 0), ("planes", "i", 1, (2, 3)),
-             ("words", "i", 0, 1), ("planes", "z", 0, (0, 1)), ("words", "z", 0, 0), ("planes", "z", 0, (2, 3)),
-             ("planes", "z", 1, (0, 1)), ("words", "z", 0, 1), ("planes", "z", 1, (2, 3)),
+             ("words", "f", 0, 1), ("planes", "i", 0, (0, 1)), ("c", 0), ("planes", "i", 0, (2, 3)), ("n", 0), ("planes", "i", 1, (0, 1)), ("words", "i", 0, 0), ("planes", "i", 1, (2, 3)), ("words", "i", 0, 1),
+             ("planes", "z", 0, (0, 1, 2, 3)), ("planes", "z", 1, (0, 1, 2, 3)), ("words", "z", 0, 0), ("words", "z", 0, 1),
              ("words", "f", 1, 0), ("words", "f", 1, 1), ("c", 1), ("n", 1),
              ("words", "i", 1, 0), ("words", "i", 1, 1), ("words", "z", 1, 0), ("words", "z", 1, 1)]
     return loads
@@ -46,10 +45,10 @@ def make_loads():
 
 def make_plan():
     plan = [("idle", 3)] if 3 else []
-    plan.extend([("turn", 0, 0), ("spread", "f"), ("bias", "f", "v"), ("turn", 0, 1), ("quant", 0, 0), ("quant", 0, 1)])
-    plan.extend([("turn", 1, 0), ("turn", 1, 1), ("spread", "i"), ("quant", 1, 0), ("quant", 1, 1), ("bias", "i", "v")])
-    plan.extend([("turn", 0, 2), ("turn", 0, 3), ("spread", "z"), ("quant", 0, 2), ("quant", 0, 3), ("bias", "z", "v")])
-    plan.extend([("turn", 1, 2), ("turn", 1, 3), ("quant", 1, 2), ("quant", 1, 3)])
+    plan.extend([("turn", 0, 0), ("spread", "f", (0,)), ("turn", 0, 1), ("spread", "f", (1,)), ("bias", "f", "v"), ("quant", 0, 0), ("quant", 0, 1)])
+    plan.extend([("turn", 1, 0), ("spread", "i", (0,)), ("turn", 1, 1), ("spread", "i", (1,)), ("quant", 1, 0), ("quant", 1, 1), ("bias", "i", "v")])
+    plan.extend([("turn", 0, 2), ("spread", "z", (0,)), ("turn", 0, 3), ("spread", "z", (1,)), ("quant", 0, 2), ("quant", 0, 3), ("bias", "z", "v")])
+    plan.extend([("turn", 1, 2), ("idle", 1), ("turn", 1, 3), ("quant", 1, 2), ("quant", 1, 3)])
     plan.extend([("xpart", bt) for bt in range(0)])
     for bt in range(B_TILES):
         plan.extend([("slot", "f", 0, bt), ("old", 0, bt)])
@@ -216,9 +215,10 @@ def tile_slstmcell_pa_kernel(
 
         wide = {}
 
-        def spread(gate):
-            wide[gate] = psum.tile([P, D_H], BF16, name="wide", tag="acc", bufs=ACC_BANKS)
-            for nch in range(N_CHUNKS):
+        def spread(gate, chunks=range(N_CHUNKS)):
+            if 0 in chunks:
+                wide[gate] = psum.tile([P, D_H], BF16, name="wide", tag="acc", bufs=ACC_BANKS)
+            for nch in chunks:
                 cols = slice(N_CHUNK * nch, N_CHUNK * (nch + 1))
                 nc.tensor.matmul(
                     out=wide[gate][:, cols],
@@ -239,15 +239,15 @@ def tile_slstmcell_pa_kernel(
             else:
                 nc.scalar.copy(out=bias[gate][:], in_=wide[gate][:])
 
-        def passes(gate, nch, bt, acc, which):
-            cols = slice(N_CHUNK * nch, N_CHUNK * (nch + 1))
+        def passes(gate, nch, bt, acc, which, part=slice(0, N_CHUNK)):
+            cols = slice(N_CHUNK * nch + part.start, N_CHUNK * nch + part.stop)
             for c in which:
                 s, g = divmod(c, HALVES)
                 nc.tensor.matmul_mx(
                     out=acc[:],
                     lhsT=act_codes[s, bt][:, P * g : P * (g + 1)].bitcast(FP8X4),
                     lhsT_scale=act_scales[s, bt][:, P * g : P * (g + 1)],
-                    rhs=w_codes[gate, nch, s][:, g, :].bitcast(FP8X4),
+                    rhs=w_codes[gate, nch, s][:, g, part].bitcast(FP8X4),
                     rhs_scale=w_planes[gate][4 * g : P, s, cols],
                     start=(c == 0),
                     stop=(c == PASSES - 1),
@@ -319,7 +319,7 @@ def tile_slstmcell_pa_kernel(
             elif step[0] == "idle":
                 idle(step[1])
             elif step[0] == "spread":
-                spread(step[1])
+                spread(*step[1:])
             elif step[0] == "bias":
                 keep_bias(step[1], len(step) > 2)
             elif step[0] == "xpart":
@@ -333,6 +333,29 @@ def tile_slstmcell_pa_kernel(
                 slot += 1
                 gate, nch, bt = step[1], step[2], step[3]
                 cols = slice(N_CHUNK * nch, N_CHUNK * (nch + 1))
+                if slot == last and SPLIT_LAST > 1:
+                    width = N_CHUNK // SPLIT_LAST
+                    parts = [slice(width * k, width * (k + 1)) for k in range(SPLIT_LAST)]
+                    pre = work.tile([P, N_CHUNK], F32, name="pre")
+                    fresh = work.tile([P, N_CHUNK], F32, name="fresh")
+                    new_c = kept_c[nch, bt]
+                    for part in parts:
+                        acc = psum.tile([P, width], F32, name="acc", tag="acc", bufs=ACC_BANKS)
+                        passes(gate, nch, bt, acc, range(PASSES), part)
+                        wide_part = slice(N_CHUNK * nch + part.start, N_CHUNK * nch + part.stop)
+                        nc.vector.tensor_tensor(out=pre[:, part], in0=acc[:], in1=bias[gate][:, wide_part], op=ADD)
+                        nc.scalar.activation(out=fresh[:, part], in_=pre[:, part], func=TANH)
+                    for emit in later.pop(slot, []):
+                        emit()
+                    for part in parts:
+                        nc.vector.tensor_tensor(out=fresh[:, part], in0=fresh[:, part], in1=in_gate[nch, bt][:, part], op=MULT)
+                    for part in parts:
+                        nc.vector.tensor_tensor(out=new_c[:, part], in0=new_c[:, part], in1=fresh[:, part], op=ADD)
+                        nc.sync.dma_start(
+                            out=out_0[P * bt : P * (bt + 1), N_CHUNK * nch + part.start : N_CHUNK * nch + part.stop],
+                            in_=new_c[:, part],
+                        )
+                    continue
                 if gate == "f" and nch == 0 and bt in open_acc:
                     acc = open_acc[bt]
                     passes(gate, nch, bt, acc, (2, 3))

from contextlib import ExitStack

from concourse import mybir
from concourse.masks import make_identity

F32 = mybir.dt.float32
BF16 = mybir.dt.bfloat16
I32 = mybir.dt.int32
U32 = mybir.dt.uint32
U8 = mybir.dt.uint8
FP8X4 = mybir.dt.float8_e4m3fn_x4
ADD = mybir.AluOpType.add
MULT = mybir.AluOpType.mult
EXP = mybir.ActivationFunctionType.Exp
TANH = mybir.ActivationFunctionType.Tanh

P = 128
BATCH = 512
D_IN = 1024
D_H = 1024
K_PASS = 512
HALVES = D_IN // K_PASS
PASSES = 2 * HALVES
B_TILES = BATCH // P
N_CHUNK = 512
N_CHUNKS = D_H // N_CHUNK
GATES = ("f", "i", "z")
ACC_BANKS = 5
AUX_BANKS = 3
C_LAG = (3, 2)
N_LAG = (1, 1)
N_ON_POOL = ()
SPLIT_LAST = 1
Z_ON_VECTOR = ()

def make_loads():
    loads = [("act", 0, 0), ("biases", GATES), ("act", 0, 1), ("acts", 1, 0), ("planes", "f", 0, (0, 1)), ("acts", 0, 1), ("planes", "f", 0, (2, 3)),
             ("acts", 1, 1), ("planes", "f", 1, (0, 1)), ("words", "f", 0, 0), ("planes", "f", 1, (2, 3)),
             ("words", "f", 0, 1), ("planes", "i", 0, (0, 1)), ("c", 0), ("planes", "i", 0, (2, 3)), ("n", 0), ("planes", "i", 1, (0, 1)), ("words", "i", 0, 0), ("planes", "i", 1, (2, 3)), ("words", "i", 0, 1),
             ("planes", "z", 0, (0, 1, 2, 3)), ("planes", "z", 1, (0, 1, 2, 3)), ("words", "z", 0, 0), ("words", "z", 0, 1),
             ("words", "f", 1, 0), ("words", "f", 1, 1), ("c", 1), ("n", 1),
             ("words", "i", 1, 0), ("words", "i", 1, 1), ("words", "z", 1, 0), ("words", "z", 1, 1)]
    return loads


def make_plan():
    plan = [("idle", 3)] if 3 else []
    plan.extend([("turn", 0, 0), ("spread", "f", (0,)), ("turn", 0, 1), ("spread", "f", (1,)), ("bias", "f", "v"), ("quant", 0, 0), ("quant", 0, 1)])
    plan.extend([("turn", 1, 0), ("spread", "i", (0,)), ("turn", 1, 1), ("spread", "i", (1,)), ("quant", 1, 0), ("quant", 1, 1), ("bias", "i", "v")])
    plan.extend([("turn", 0, 2), ("spread", "z", (0,)), ("turn", 0, 3), ("spread", "z", (1,)), ("quant", 0, 2), ("quant", 0, 3), ("bias", "z", "v")])
    plan.extend([("turn", 1, 2), ("idle", 1), ("turn", 1, 3), ("quant", 1, 2), ("quant", 1, 3)])
    plan.extend([("xpart", bt) for bt in range(0)])
    for bt in range(B_TILES):
        plan.extend([("slot", "f", 0, bt), ("old", 0, bt)])
    plan.extend([("slot", "i", 0, bt) for bt in range(B_TILES)])
    plan.extend([("slot", "z", 0, bt) for bt in range(B_TILES)])
    for bt in range(B_TILES):
        plan.extend([("slot", "f", 1, bt), ("old", 1, bt)])
    for bt in range(B_TILES):
        plan.extend([("slot", "i", 1, bt), ("slot", "z", 1, bt)])
    return plan


FLOPS = 2 * BATCH * (2 * D_IN) * (3 * D_H)


def tile_slstmcell_pa_kernel(
    tc,
    x, h_prev, c_prev, n_prev,
    W_i_words, W_i_scales, b_i, U_i_words, U_i_scales,
    W_f_words, W_f_scales, b_f, U_f_words, U_f_scales,
    W_z_words, W_z_scales, b_z, U_z_words, U_z_scales,
    out_0, out_1,
):
    nc = tc.nc
    words_of = {"i": (W_i_words, U_i_words), "f": (W_f_words, U_f_words), "z": (W_z_words, U_z_words)}
    scales_of = {"i": (W_i_scales, U_i_scales), "f": (W_f_scales, U_f_scales), "z": (W_z_scales, U_z_scales)}
    bias_of = {"i": b_i, "f": b_f, "z": b_z}

    with ExitStack() as stack:
        keep = stack.enter_context(tc.tile_pool(name="keep", bufs=1))
        stage = stack.enter_context(tc.tile_pool(name="stage", bufs=4))
        work = stack.enter_context(tc.tile_pool(name="work", bufs=4))
        hold = stack.enter_context(tc.tile_pool(name="hold", bufs=2 * B_TILES))
        psum = stack.enter_context(tc.psum_pool(name="psum", bufs=1))

        ident = keep.tile([P, P], F32, name="ident")
        ident_bf = keep.tile([P, P], BF16, name="ident_bf")
        warm = keep.tile([P, 2], F32, name="warm")
        zeros = keep.tile([P, N_CHUNK], BF16, name="zeros")
        bias_rows = keep.tile([P, N_CHUNK], BF16, name="bias_rows")
        raw = {}
        act_codes = {}
        act_scales = {}
        for s in range(2):
            for pair in range(B_TILES // 2):
                raw[s, pair] = keep.tile([P, 2, D_IN], BF16, name="raw%d%d" % (s, pair))
            for bt in range(B_TILES):
                act_codes[s, bt] = keep.tile([P, HALVES * P], U32, name="ac%d%d" % (s, bt), align_bytes=64)
                act_scales[s, bt] = keep.tile([P, HALVES * P], U8, name="as%d%d" % (s, bt), align_bytes=64)
        w_codes = {}
        for gate in GATES:
            for nch in range(N_CHUNKS):
                for s in range(2):
                    w_codes[gate, nch, s] = keep.tile(
                        [P, HALVES, N_CHUNK], U32, name="w_%s%d%d" % (gate, nch, s), align_bytes=64
                    )
        w_planes = {g: keep.tile([P, 2, D_H], U8, name="planes_%s" % g, align_bytes=64) for g in GATES}
        bias = {g: keep.tile([P, D_H], BF16, name="bias_%s" % g) for g in GATES}
        prev_c = [keep.tile([P, B_TILES, N_CHUNK], BF16, name="prev_c%d" % nch) for nch in range(N_CHUNKS)]
        prev_n = [keep.tile([P, B_TILES, N_CHUNK], BF16, name="prev_n%d" % nch) for nch in range(N_CHUNKS)]

        nc.vector.memset(bias_rows[:].bitcast(I32), 0)
        nc.vector.memset(zeros[:].bitcast(I32), 0)
        nc.vector.memset(warm[:, 0:1], 0.0)
        nc.vector.memset(w_planes[GATES[0]][:].rearrange("p s n -> p (s n)").bitcast(I32), 0)
        for gate in GATES[1:]:
            nc.vector.memset(w_planes[gate][:].rearrange("p s n -> p (s n)").bitcast(I32), 0)
        make_identity(nc, ident_bf[:])
        make_identity(nc, ident[:])

        stack.enter_context(tc.manual_schedule())

        nc.scalar.activation(out=warm[:, 1:2], in_=warm[:, 0:1], func=EXP)

        def load_acts(s, pair):
            source = (x, h_prev)[s]
            nc.sync.dma_start(
                out=raw[s, pair][:],
                in_=source[2 * P * pair : 2 * P * (pair + 1), :].rearrange("(bt p) k -> p bt k", p=P),
            )

        def load_act_tile(s, bt):
            nc.sync.dma_start(
                out=raw[s, bt // 2][:, bt % 2, :], in_=(x, h_prev)[s][P * bt : P * (bt + 1), :]
            )

        def load_biases(gates):
            for gate in gates:
                gi = GATES.index(gate)
                nc.sync.dma_start(
                    out=bias_rows[N_CHUNKS * gi : N_CHUNKS * (gi + 1), :],
                    in_=bias_of[gate].rearrange("(o n) -> o n", o=N_CHUNKS),
                )

        def load_wide_bias(gate):
            nc.sync.dma_start(out=bias[gate][:], in_=bias_of[gate].partition_broadcast(P))

        def load_planes(gate, s, quads):
            for quad in quads:
                nc.sync.dma_start(
                    out=w_planes[gate][32 * quad : 32 * quad + 4 * HALVES, s, :].bitcast(I32),
                    in_=scales_of[gate][s][:, 4 * quad : 4 * quad + 4, :].bitcast(I32),
                )

        def load_words(gate, nch, s):
            by_partition = words_of[gate][s].rearrange("g p n t -> p g (n t)")
            nc.sync.dma_start(
                out=w_codes[gate, nch, s][:].bitcast(I32),
                in_=by_partition[:, :, 4 * N_CHUNK * nch : 4 * N_CHUNK * (nch + 1)].bitcast(I32),
            )

        def load_prev(tile_, source, nch):
            cols = slice(N_CHUNK * nch, N_CHUNK * (nch + 1))
            nc.sync.dma_start(out=tile_[:], in_=source.rearrange("(bt p) n -> p bt n", p=P)[:, :, cols])

        for step in make_loads():
            if step[0] == "acts":
                load_acts(step[1], step[2])
            elif step[0] == "act":
                load_act_tile(step[1], step[2])
            elif step[0] == "biases":
                load_biases(step[1])
            elif step[0] == "wide_bias":
                load_wide_bias(step[1])
            elif step[0] == "planes":
                load_planes(step[1], step[2], step[3])
            elif step[0] == "words":
                load_words(step[1], step[2], step[3])
            elif step[0] == "c":
                load_prev(prev_c[step[1]], c_prev, step[1])
            else:
                load_prev(prev_n[step[1]], n_prev, step[1])

        sorted_of = {}
        grouped_of = {}

        def sort_words(s, bt):
            pairs = raw[s, bt // 2][:, bt % 2, :].bitcast(F32)
            sorted_of[s, bt] = stage.tile([P, HALVES * 2, P], F32, name="sorted_words")
            nc.vector.tensor_copy(
                out=sorted_of[s, bt][:].rearrange("p (g u) w -> p g u w", u=2),
                in_=pairs.rearrange("p (g w u) -> p g u w", g=HALVES, u=2),
            )

        def turn(s, bt):
            words = raw[s, bt // 2][:, bt % 2, :].bitcast(F32)
            turned = psum.tile([P, HALVES * 2, P], F32, name="turned", tag="aux", bufs=AUX_BANKS)
            for gu in range(HALVES * 2):
                g, u = divmod(gu, 2)
                nc.tensor.transpose(turned[:, gu, :], words[:, 2 * P * g + u : 2 * P * (g + 1) : 2], ident[:])
            grouped = stage.tile([P, HALVES, P, 4], BF16, name="grouped", align_bytes=64)
            nc.scalar.copy(
                out=grouped[:].bitcast(F32),
                in_=turned[:].rearrange("p (g u) b -> p g b u", u=2),
            )
            grouped_of[s, bt] = grouped

        def quantise(s, bt):
            nc.vector.quantize_mx(
                out=act_codes[s, bt][:].bitcast(FP8X4),
                scales=act_scales[s, bt][:],
                in_=grouped_of[s, bt][:].rearrange("p g b t -> p (g b t)"),
            )

        wide = {}

        def spread(gate, chunks=range(N_CHUNKS)):
            if 0 in chunks:
                wide[gate] = psum.tile([P, D_H], BF16, name="wide", tag="acc", bufs=ACC_BANKS)
            for nch in chunks:
                cols = slice(N_CHUNK * nch, N_CHUNK * (nch + 1))
                nc.tensor.matmul(
                    out=wide[gate][:, cols],
                    lhsT=ident_bf[:, N_CHUNKS * GATES.index(gate) + nch : N_CHUNKS * GATES.index(gate) + nch + 1].to_broadcast([P, P]),
                    rhs=bias_rows[:],
                    start=True,
                    stop=True,
                )

        def idle(count):
            scratch = psum.tile([P, N_CHUNK], F32, name="scratch", tag="acc", bufs=ACC_BANKS)
            for turn_no in range(count):
                nc.tensor.matmul(out=scratch[:], lhsT=zeros[:, 0:P], rhs=zeros[:], start=True, stop=True)

        def keep_bias(gate, on_vector):
            if on_vector:
                nc.vector.tensor_copy(out=bias[gate][:], in_=wide[gate][:])
            else:
                nc.scalar.copy(out=bias[gate][:], in_=wide[gate][:])

        def passes(gate, nch, bt, acc, which, part=slice(0, N_CHUNK)):
            cols = slice(N_CHUNK * nch + part.start, N_CHUNK * nch + part.stop)
            for c in which:
                s, g = divmod(c, HALVES)
                nc.tensor.matmul_mx(
                    out=acc[:],
                    lhsT=act_codes[s, bt][:, P * g : P * (g + 1)].bitcast(FP8X4),
                    lhsT_scale=act_scales[s, bt][:, P * g : P * (g + 1)],
                    rhs=w_codes[gate, nch, s][:, g, part].bitcast(FP8X4),
                    rhs_scale=w_planes[gate][4 * g : P, s, cols],
                    start=(c == 0),
                    stop=(c == PASSES - 1),
                )

        later = {}
        kept_c = {}
        kept_n = {}
        in_gate = {}
        forget_of = {}
        old_of = {}
        plan = make_plan()
        slots = [step for step in plan if step[0] == "slot"]
        last = len(slots) - 1

        def f_products(nch, bt):
            def emit():
                kept_c[nch, bt] = hold.tile([P, N_CHUNK], F32, name="kept_c")
                kept_n[nch, bt] = hold.tile([P, N_CHUNK], F32, name="kept_n")
                nc.vector.tensor_tensor(
                    out=kept_c[nch, bt][:],
                    in0=forget_of[nch, bt][:],
                    in1=old_of[nch, bt][:] if (nch, bt) in old_of else prev_c[nch][:, bt, :],
                    op=MULT,
                )
                nc.gpsimd.tensor_tensor(
                    out=kept_n[nch, bt][:], in0=forget_of[nch, bt][:], in1=prev_n[nch][:, bt, :], op=MULT
                )
            return emit

        def finish_n(nch, bt):
            def emit():
                new_n = kept_n[nch, bt]
                (nc.gpsimd if (nch, bt) in N_ON_POOL else nc.vector).tensor_tensor(out=new_n[:], in0=new_n[:], in1=in_gate[nch, bt][:], op=ADD)
                nc.sync.dma_start(
                    out=out_1[P * bt : P * (bt + 1), N_CHUNK * nch : N_CHUNK * (nch + 1)], in_=new_n[:]
                )
            return emit

        def fresh_product(engine, nch, bt, fresh):
            def emit():
                engine.tensor_tensor(out=fresh[:], in0=fresh[:], in1=in_gate[nch, bt][:], op=MULT)
            return emit

        def finish_c(engine, nch, bt, fresh):
            def emit():
                new_c = kept_c[nch, bt]
                engine.tensor_tensor(out=new_c[:], in0=new_c[:], in1=fresh[:], op=ADD)
                nc.sync.dma_start(
                    out=out_0[P * bt : P * (bt + 1), N_CHUNK * nch : N_CHUNK * (nch + 1)], in_=new_c[:]
                )
            return emit

        def lay_old(nch, bt):
            old_of[nch, bt] = psum.tile([P, N_CHUNK], F32, name="old", tag="aux", bufs=AUX_BANKS)
            nc.tensor.matmul(
                out=old_of[nch, bt][:], lhsT=ident_bf[:], rhs=prev_c[nch][:, bt, :], start=True, stop=True
            )

        slot = -1
        open_acc = {}
        for step in plan:
            if step[0] == "sort":
                sort_words(step[1], step[2])
            elif step[0] == "turn":
                turn(step[1], step[2])
            elif step[0] == "quant":
                quantise(step[1], step[2])
            elif step[0] == "idle":
                idle(step[1])
            elif step[0] == "spread":
                spread(*step[1:])
            elif step[0] == "bias":
                keep_bias(step[1], len(step) > 2)
            elif step[0] == "xpart":
                open_acc[step[1]] = psum.tile([P, N_CHUNK], F32, name="acc", tag="acc", bufs=ACC_BANKS)
                passes("f", 0, step[1], open_acc[step[1]], (0, 1))
            elif step[0] in ("old", "plain"):
                if step[0] == "old":
                    lay_old(step[1], step[2])
                later.setdefault(slot + 1, []).append(f_products(step[1], step[2]))
            else:
                slot += 1
                gate, nch, bt = step[1], step[2], step[3]
                cols = slice(N_CHUNK * nch, N_CHUNK * (nch + 1))
                if slot == last and SPLIT_LAST > 1:
                    width = N_CHUNK // SPLIT_LAST
                    parts = [slice(width * k, width * (k + 1)) for k in range(SPLIT_LAST)]
                    pre = work.tile([P, N_CHUNK], F32, name="pre")
                    fresh = work.tile([P, N_CHUNK], F32, name="fresh")
                    new_c = kept_c[nch, bt]
                    for part in parts:
                        acc = psum.tile([P, width], F32, name="acc", tag="acc", bufs=ACC_BANKS)
                        passes(gate, nch, bt, acc, range(PASSES), part)
                        wide_part = slice(N_CHUNK * nch + part.start, N_CHUNK * nch + part.stop)
                        nc.vector.tensor_tensor(out=pre[:, part], in0=acc[:], in1=bias[gate][:, wide_part], op=ADD)
                        nc.scalar.activation(out=fresh[:, part], in_=pre[:, part], func=TANH)
                    for emit in later.pop(slot, []):
                        emit()
                    for part in parts:
                        nc.vector.tensor_tensor(out=fresh[:, part], in0=fresh[:, part], in1=in_gate[nch, bt][:, part], op=MULT)
                    for part in parts:
                        nc.vector.tensor_tensor(out=new_c[:, part], in0=new_c[:, part], in1=fresh[:, part], op=ADD)
                        nc.sync.dma_start(
                            out=out_0[P * bt : P * (bt + 1), N_CHUNK * nch + part.start : N_CHUNK * nch + part.stop],
                            in_=new_c[:, part],
                        )
                    continue
                if gate == "f" and nch == 0 and bt in open_acc:
                    acc = open_acc[bt]
                    passes(gate, nch, bt, acc, (2, 3))
                else:
                    acc = psum.tile([P, N_CHUNK], F32, name="acc", tag="acc", bufs=ACC_BANKS)
                    passes(gate, nch, bt, acc, range(PASSES))
                pre = work.tile([P, N_CHUNK], F32, name="pre")
                nc.vector.tensor_tensor(out=pre[:], in0=acc[:], in1=bias[gate][:, cols], op=ADD)
                if gate == "f":
                    forget_of[nch, bt] = work.tile([P, N_CHUNK], F32, name="forget")
                    nc.scalar.activation(out=forget_of[nch, bt][:], in_=pre[:], func=EXP)
                elif gate == "i":
                    in_gate[nch, bt] = work.tile([P, N_CHUNK], F32, name="in_gate")
                    nc.scalar.activation(out=in_gate[nch, bt][:], in_=pre[:], func=EXP)
                    later.setdefault(slot + N_LAG[nch], []).append(finish_n(nch, bt))
                else:
                    fresh = work.tile([P, N_CHUNK], F32, name="fresh")
                    nc.scalar.activation(out=fresh[:], in_=pre[:], func=TANH)
                    if slot == last:
                        later.setdefault(slot + 1, []).append(fresh_product(nc.vector, nch, bt, fresh))
                        later.setdefault(slot + 1, []).append(finish_c(nc.vector, nch, bt, fresh))
                    else:
                        later.setdefault(slot + 1, []).append(fresh_product(nc.vector if (nch, bt) in Z_ON_VECTOR else nc.gpsimd, nch, bt, fresh))
                        later.setdefault(slot + C_LAG[nch], []).append(finish_c(nc.vector, nch, bt, fresh))
                for emit in later.get(slot, []):
                    emit()
        for rest in range(last + 1, last + 5):
            for emit in later.get(rest, []):
                emit()
